import numpy as np
import ml_dtypes


def mxq(x, axis, fmt="e4m3"):
    dtype, down = {"e4m3": (ml_dtypes.float8_e4m3fn, 7), "e5m2": (ml_dtypes.float8_e5m2, 14)}[fmt]
    v = np.moveaxis(np.asarray(x, np.float32).astype(ml_dtypes.bfloat16).astype(np.float64), axis, -1)
    blocks = v.reshape(v.shape[:-1] + (-1, 32))
    amax = np.abs(blocks).max(-1, keepdims=True)
    byte = np.maximum(np.where(amax > 0, np.frexp(amax)[1] - 1 + 127, 0) - down, 1)
    scale = np.exp2(byte - 127.0)
    codes = (blocks / scale).astype(np.float32).astype(dtype).astype(np.float64)
    return np.moveaxis((codes * scale).reshape(v.shape), -1, axis)


WIDE = False


def mx_kscale(k):
    if not WIDE:
        return np.ones(k)
    levels = np.array([10, -10, 5, -5, 0])
    a = np.random.permutation(np.resize(levels, k // 512 * 4)).reshape(k // 512, 4)
    idx = np.arange(k)
    return np.exp2(a[idx // 512, idx % 128 // 32])


BF16 = ml_dtypes.bfloat16


def bf(x):
    return np.asarray(x, np.float32).astype(BF16)


def f64(x):
    return np.asarray(x).astype(np.float64)


B, C, T, F, H, D = 1, 128, 512, 32, 4, 64
K = D * F
EPS = 1e-5


def conv_prelu_tln(x, W, b, a, lw, lb):
    y = (f64(W).reshape(H * D, C) @ f64(x).reshape(B, C, T * F)).reshape(B, H, D, T, F)
    y = y + f64(b)[None, :, :, None, None]
    y = np.where(y >= 0, y, f64(a)[None, :, None, None, None] * y)
    mu = y.mean(axis=(2, -1), keepdims=True)
    var = np.square(y - mu).mean(axis=(2, -1), keepdims=True)
    y = (y - mu) / np.sqrt(var + EPS)
    y = y * f64(lw)[None, :, :, None, :] + f64(lb)[None, :, :, None, :]
    return np.swapaxes(y, 2, 3).reshape(B, H, T, K)


def setup_inputs():
    n = np.random.standard_normal
    s = mx_kscale(K).reshape(D, F)
    return {"x": bf(n((B, C, T, F))),
            "Wq": bf(n((H, D, C)) / np.sqrt(C)), "bq": bf(0.2 * n((H, D))), "aq": bf(0.25 + 0.05 * n(H)),
            "lwq": bf((1.0 + 0.1 * n((H, D, F))) * s), "lbq": bf(0.2 * n((H, D, F)) * s),
            "Wk": bf(n((H, D, C)) / np.sqrt(C)), "bk": bf(0.2 * n((H, D))), "ak": bf(0.25 + 0.05 * n(H)),
            "lwk": bf((1.0 + 0.1 * n((H, D, F))) / s), "lbk": bf(0.2 * n((H, D, F)) / s)}


def reference(x, Wq, bq, aq, lwq, lbq, Wk, bk, ak, lwk, lbk):
    qf = conv_prelu_tln(x, Wq, bq, aq, lwq, lbq)
    kf = conv_prelu_tln(x, Wk, bk, ak, lwk, lbk)
    return (mxq(qf, 3, "e4m3") @ mxq(kf, 3, "e4m3").transpose(0, 1, 3, 2)) * (1.0 / np.sqrt(K))

@@ -1,0 +1,266 @@
+import math
+from contextlib import ExitStack
+
+import concourse.mybir as mybir
+from concourse.masks import make_identity
+
+F32 = mybir.dt.float32
+BF16 = mybir.dt.bfloat16
+U32 = mybir.dt.uint32
+U8 = mybir.dt.uint8
+FP8X4 = mybir.dt.float8_e4m3fn_x4
+ALU = mybir.AluOpType
+ACT = mybir.ActivationFunctionType
+
+P = 128
+C = 128
+T = 512
+F = 32
+H = 4
+D = 64
+K = D * F
+EPS = 1e-5
+G = 2 * H
+FRAME_TILES = T // P
+PACK = 4
+K_PASS = P * PACK
+PASSES = K // K_PASS
+OCT = F // PACK
+
+FLOPS = 2 * C * (G * D) * (T * F) + 2 * H * T * T * K
+
+
+def tile_multiheadselfattention_pa_kernel(
+    tc, x, Wq, bq, aq, lwq, lbq, Wk, bk, ak, lwk, lbk, out
+):
+    nc = tc.nc
+    with ExitStack() as ctx:
+        const = ctx.enter_context(tc.tile_pool(name="const", bufs=1))
+        raw_pool = ctx.enter_context(tc.tile_pool(name="raw", bufs=2))
+        feat_pool = ctx.enter_context(tc.tile_pool(name="feat", bufs=2))
+        stat_pool = ctx.enter_context(tc.tile_pool(name="stat", bufs=4))
+        work_pool = ctx.enter_context(tc.tile_pool(name="work", bufs=2))
+        code_pool = ctx.enter_context(tc.tile_pool(name="code", bufs=4))
+        out_pool = ctx.enter_context(tc.tile_pool(name="outp", bufs=3))
+        conv_psum = ctx.enter_context(tc.psum_pool(name="convp", bufs=3))
+        turn_psum = ctx.enter_context(tc.psum_pool(name="turnp", bufs=3))
+        score_psum = ctx.enter_context(tc.psum_pool(name="scorep", bufs=2))
+
+        ident_f32 = const.tile([P, P], F32)
+        make_identity(nc, ident_f32[:])
+        ident_bf = const.tile([P, P], BF16)
+        make_identity(nc, ident_bf[:])
+        eps_col = const.tile([P, 1], F32)
+        nc.vector.memset(eps_col[:], EPS)
+
+        slope_q = const.tile([P, H], BF16)
+        nc.scalar.dma_start(out=slope_q[:], in_=aq.partition_broadcast(P))
+        slope_k = const.tile([P, H], BF16)
+        nc.scalar.dma_start(out=slope_k[:], in_=ak.partition_broadcast(P))
+        slope = const.tile([P, G], F32)
+        nc.vector.tensor_copy(out=slope[:, 0:H], in_=slope_q[:])
+        nc.vector.tensor_copy(out=slope[:, H:G], in_=slope_k[:])
+
+        sign = const.tile([P, G], F32)
+        nc.vector.tensor_scalar(
+            out=sign[:], in0=slope[:], scalar1=1.0, scalar2=-2.0, op0=ALU.is_gt, op1=ALU.mult
+        )
+        nc.vector.tensor_scalar_add(out=sign[:], in0=sign[:], scalar1=1.0)
+
+        w_rows = const.tile([P, 4, C], BF16)
+        nc.sync.dma_start(out=w_rows[:, 0:2, :], in_=Wq.rearrange("(a h) d c -> (h d) a c", a=2))
+        nc.sync.dma_start(out=w_rows[:, 2:4, :], in_=Wk.rearrange("(a h) d c -> (h d) a c", a=2))
+        w_turned = turn_psum.tile([P, 4, P], BF16, tag="turned")
+        for i in range(4):
+            nc.tensor.transpose(w_turned[:, i, :], w_rows[:, i, :], ident_bf[:])
+        w_T = const.tile([P, G, D], BF16)
+        nc.vector.tensor_tensor(
+            out=w_T[:],
+            in0=w_turned[:].rearrange("c i (h d) -> c (i h) d", d=D),
+            in1=sign[:].unsqueeze(2).to_broadcast([P, G, D]),
+            op=ALU.mult,
+        )
+
+        x_pairs = const.tile([P, (F // 2) * T * 2], BF16)
+        x_words = x_pairs[:].bitcast(F32).rearrange("c (w t) -> c w t", t=T)
+        x_cols = x_pairs[:].rearrange("c (w t e) -> c w t e", t=T, e=2)
+        for tt in range(FRAME_TILES):
+            frames = slice(tt * P, (tt + 1) * P)
+            x_raw = raw_pool.tile([P, P * F], BF16)
+            nc.sync.dma_start(out=x_raw[:], in_=x[0, :, frames, :].rearrange("c t f -> c (t f)"))
+            nc.vector.tensor_copy(
+                out=x_words[:, :, frames],
+                in_=x_raw[:].bitcast(F32).rearrange("c (t w) -> c w t", w=F // 2),
+            )
+
+        bias_q = const.tile([P, H, D], BF16)
+        nc.scalar.dma_start(
+            out=bias_q[:].rearrange("p h d -> p (h d)"),
+            in_=bq.rearrange("h d -> (h d)").partition_broadcast(P),
+        )
+        bias_k = const.tile([P, H, D], BF16)
+        nc.scalar.dma_start(
+            out=bias_k[:].rearrange("p h d -> p (h d)"),
+            in_=bk.rearrange("h d -> (h d)").partition_broadcast(P),
+        )
+        bias = const.tile([P, G, D], F32)
+        nc.vector.tensor_tensor(
+            out=bias[:, 0:H, :],
+            in0=bias_q[:],
+            in1=sign[:, 0:H].unsqueeze(2).to_broadcast([P, H, D]),
+            op=ALU.mult,
+        )
+        nc.vector.tensor_tensor(
+            out=bias[:, H:G, :],
+            in0=bias_k[:],
+            in1=sign[:, H:G].unsqueeze(2).to_broadcast([P, H, D]),
+            op=ALU.mult,
+        )
+
+        gain_rows_bf = const.tile([P, P], BF16)
+        shift_rows_bf = const.tile([P, P], BF16)
+        for side, (lw, lb) in enumerate(((lwq, lbq), (lwk, lbk))):
+            for rows_bf, table in ((gain_rows_bf, lw), (shift_rows_bf, lb)):
+                by_j = table.rearrange("h (s d) (j f) -> j (h s) d f", s=PASSES, j=PACK)
+                for j in range(PACK):
+                    nc.scalar.dma_start(
+                        out=rows_bf[side * 64 + j : (side + 1) * 64 : PACK, :].rearrange(
+                            "r (d f) -> r d f", f=OCT
+                        ),
+                        in_=by_j[j],
+                    )
+        gain_rows = const.tile([P, P], F32)
+        nc.vector.tensor_copy(out=gain_rows[:], in_=gain_rows_bf[:])
+        shift_rows = const.tile([P, P], F32)
+        nc.vector.tensor_copy(out=shift_rows[:], in_=shift_rows_bf[:])
+        table_turned = turn_psum.tile([P, 2, P], F32, tag="turned")
+        nc.tensor.transpose(table_turned[:, 0, :], gain_rows[:], ident_f32[:])
+        nc.tensor.transpose(table_turned[:, 1, :], shift_rows[:], ident_f32[:])
+        gain_T = const.tile([P, G, PASSES * PACK], F32)
+        nc.vector.tensor_tensor(
+            out=gain_T[:],
+            in0=table_turned[:, 0, :].rearrange("p (g c) -> p g c", g=G),
+            in1=sign[:].unsqueeze(2).to_broadcast([P, G, PASSES * PACK]),
+            op=ALU.mult,
+        )
+        shift_T = const.tile([P, G, PASSES * PACK], F32)
+        nc.vector.tensor_copy(
+            out=shift_T[:], in_=table_turned[:, 1, :].rearrange("p (g c) -> p g c", g=G)
+        )
+
+        def quantised_features(g):
+            feat = feat_pool.tile([P, FRAME_TILES, K], F32)
+            total = stat_pool.tile([P, FRAME_TILES], F32)
+            for tt in range(FRAME_TILES):
+                frames = slice(tt * P, (tt + 1) * P)
+                for j in range(PACK):
+                    conv = conv_psum.tile([P, OCT, D], F32)
+                    for f8 in range(OCT):
+                        f = j * OCT + f8
+                        nc.tensor.matmul(
+                            out=conv[:, f8, :],
+                            lhsT=x_cols[:, f // 2, frames, f % 2],
+                            rhs=w_T[:, g, :],
+                            start=True,
+                            stop=True,
+                        )
+                    nc.vector.tensor_tensor(
+                        out=feat[:, tt, j * K_PASS : (j + 1) * K_PASS].rearrange(
+                            "p (d f) -> p d f", f=OCT
+                        ),
+                        in0=conv[:].rearrange("p f d -> p d f"),
+                        in1=bias[:, g, :].unsqueeze(2).to_broadcast([P, D, OCT]),
+                        op=ALU.add,
+                    )
+                nc.vector.scalar_tensor_tensor(
+                    out=feat[:, tt, :],
+                    in0=feat[:, tt, :],
+                    scalar=slope[:, g : g + 1],
+                    in1=feat[:, tt, :],
+                    op0=ALU.mult,
+                    op1=ALU.max,
+                    accum_out=total[:, tt : tt + 1],
+                )
+
+            neg_mean = stat_pool.tile([P, FRAME_TILES], F32)
+            nc.vector.tensor_scalar_mul(out=neg_mean[:], in0=total[:], scalar1=-1.0 / K)
+            sq_total = stat_pool.tile([P, FRAME_TILES], F32)
+            for tt in range(FRAME_TILES):
+                squares = work_pool.tile([P, K], BF16)
+                nc.scalar.activation(
+                    out=squares[:],
+                    in_=feat[:, tt, :],
+                    func=ACT.Square,
+                    bias=neg_mean[:, tt : tt + 1],
+                    scale=1.0,
+                    accum_out=sq_total[:, tt : tt + 1],
+                )
+            std = stat_pool.tile([P, FRAME_TILES], F32)
+            nc.scalar.activation(
+                out=std[:], in_=sq_total[:], func=ACT.Sqrt, bias=eps_col[:, 0:1], scale=1.0 / K
+            )
+            rstd = stat_pool.tile([P, FRAME_TILES], F32)
+            nc.vector.reciprocal(out=rstd[:], in_=std[:])
+            offset = stat_pool.tile([P, FRAME_TILES], F32)
+            nc.vector.tensor_mul(out=offset[:], in0=neg_mean[:], in1=rstd[:])
+            for tt in range(FRAME_TILES):
+                nc.scalar.activation(
+                    out=feat[:, tt, :],
+                    in_=feat[:, tt, :],
+                    func=ACT.Identity,
+                    bias=offset[:, tt : tt + 1],
+                    scale=rstd[:, tt : tt + 1],
+                )
+
+            codes = code_pool.tile([P, PASSES, T], U32, align_bytes=64)
+            scales = code_pool.tile([P, PASSES, T], U8, align_bytes=64)
+            for s in range(PASSES):
+                planes = work_pool.tile([P, PACK, T], BF16)
+                for j in range(PACK):
+                    turned = turn_psum.tile([P, T], F32)
+                    first = j * K_PASS + s * P
+                    for tt in range(FRAME_TILES):
+                        nc.tensor.transpose(
+                            turned[:, tt * P : (tt + 1) * P],
+                            feat[:, tt, first : first + P],
+                            ident_f32[:],
+                        )
+                    col = s * PACK + j
+                    nc.scalar.activation(
+                        out=planes[:, j, :],
+                        in_=turned[:],
+                        func=ACT.Identity,
+                        bias=shift_T[:, g, col : col + 1],
+                        scale=gain_T[:, g, col : col + 1],
+                    )
+                grouped = work_pool.tile([P, T, PACK], BF16, align_bytes=64)
+                nc.vector.tensor_copy(
+                    out=grouped[:].rearrange("p (c i) j -> p c j i", i=4),
+                    in_=planes[:].rearrange("p j (c i) -> p c j i", i=4),
+                )
+                nc.vector.quantize_mx(
+                    out=codes[:, s, :].bitcast(FP8X4),
+                    scales=scales[:, s, :],
+                    in_=grouped[:].rearrange("p t j -> p (t j)"),
+                )
+            return codes, scales
+
+        for h in range(H):
+            q_codes, q_scales = quantised_features(h)
+            k_codes, k_scales = quantised_features(H + h)
+            for tt in range(FRAME_TILES):
+                frames = slice(tt * P, (tt + 1) * P)
+                acc = score_psum.tile([P, T], F32)
+                for s in range(PASSES):
+                    nc.tensor.matmul_mx(
+                        out=acc[:],
+                        lhsT=q_codes[:, s, frames].bitcast(FP8X4),
+                        lhsT_scale=q_scales[:, s, frames],
+                        rhs=k_codes[:, s, :].bitcast(FP8X4),
+                        rhs_scale=k_scales[:, s, :],
+                        start=(s == 0),
+                        stop=(s == PASSES - 1),
+                    )
+                scaled = out_pool.tile([P, T], F32)
+                nc.vector.tensor_scalar_mul(out=scaled[:], in0=acc[:], scalar1=1.0 / math.sqrt(K))
+                nc.sync.dma_start(out=out[0, h, frames, :], in_=scaled[:])

@@ -37,7 +37,7 @@ def tile_multiheadselfattention_pa_kernel(
     with ExitStack() as ctx:
         const = ctx.enter_context(tc.tile_pool(name="const", bufs=1))
         raw_pool = ctx.enter_context(tc.tile_pool(name="raw", bufs=2))
-        feat_pool = ctx.enter_context(tc.tile_pool(name="feat", bufs=2))
+        feat_pool = ctx.enter_context(tc.tile_pool(name="feat", bufs=3))
         stat_pool = ctx.enter_context(tc.tile_pool(name="stat", bufs=4))
         work_pool = ctx.enter_context(tc.tile_pool(name="work", bufs=2))
         code_pool = ctx.enter_context(tc.tile_pool(name="code", bufs=4))
@@ -50,8 +50,8 @@ def tile_multiheadselfattention_pa_kernel(
         make_identity(nc, ident_f32[:])
         ident_bf = const.tile([P, P], BF16)
         make_identity(nc, ident_bf[:])
-        eps_col = const.tile([P, 1], F32)
-        nc.vector.memset(eps_col[:], EPS)
+        minus_half = const.tile([P, FRAME_TILES], F32)
+        nc.vector.memset(minus_half[:], -0.5)
 
         slope_q = const.tile([P, H], BF16)
         nc.scalar.dma_start(out=slope_q[:], in_=aq.partition_broadcast(P))
@@ -182,8 +182,6 @@ def tile_multiheadselfattention_pa_kernel(
                     accum_out=total[:, tt : tt + 1],
                 )
 
-            neg_mean = stat_pool.tile([P, FRAME_TILES], F32)
-            nc.vector.tensor_scalar_mul(out=neg_mean[:], in0=total[:], scalar1=-1.0 / K)
             sq_total = stat_pool.tile([P, FRAME_TILES], F32)
             for tt in range(FRAME_TILES):
                 squares = work_pool.tile([P, K], BF16)
@@ -191,25 +189,28 @@ def tile_multiheadselfattention_pa_kernel(
                     out=squares[:],
                     in_=feat[:, tt, :],
                     func=ACT.Square,
-                    bias=neg_mean[:, tt : tt + 1],
-                    scale=1.0,
+                    bias=total[:, tt : tt + 1],
+                    scale=-1.0 * K,
                     accum_out=sq_total[:, tt : tt + 1],
                 )
-            std = stat_pool.tile([P, FRAME_TILES], F32)
-            nc.scalar.activation(
-                out=std[:], in_=sq_total[:], func=ACT.Sqrt, bias=eps_col[:, 0:1], scale=1.0 / K
+            neg_mean = stat_pool.tile([P, FRAME_TILES], F32)
+            nc.gpsimd.tensor_scalar(
+                out=neg_mean[:], in0=total[:], scalar1=-1.0 / K, scalar2=0.0, op0=ALU.mult, op1=ALU.add
+            )
+            var_eps = stat_pool.tile([P, FRAME_TILES], F32)
+            nc.gpsimd.tensor_scalar(
+                out=var_eps[:], in0=sq_total[:], scalar1=1.0 / (K * K * K), scalar2=EPS, op0=ALU.mult, op1=ALU.add
             )
             rstd = stat_pool.tile([P, FRAME_TILES], F32)
-            nc.vector.reciprocal(out=rstd[:], in_=std[:])
-            offset = stat_pool.tile([P, FRAME_TILES], F32)
-            nc.vector.tensor_mul(out=offset[:], in0=neg_mean[:], in1=rstd[:])
+            nc.gpsimd.tensor_tensor(out=rstd[:], in0=var_eps[:], in1=minus_half[:], op=ALU.pow)
             for tt in range(FRAME_TILES):
-                nc.scalar.activation(
+                nc.gpsimd.tensor_scalar(
                     out=feat[:, tt, :],
-                    in_=feat[:, tt, :],
-                    func=ACT.Identity,
-                    bias=offset[:, tt : tt + 1],
-                    scale=rstd[:, tt : tt + 1],
+                    in0=feat[:, tt, :],
+                    scalar1=neg_mean[:, tt : tt + 1],
+                    scalar2=rstd[:, tt : tt + 1],
+                    op0=ALU.add,
+                    op1=ALU.mult,
                 )
 
             codes = code_pool.tile([P, PASSES, T], U32, align_bytes=64)
@@ -234,10 +235,16 @@ def tile_multiheadselfattention_pa_kernel(
                         scale=gain_T[:, g, col : col + 1],
                     )
                 grouped = work_pool.tile([P, T, PACK], BF16, align_bytes=64)
-                nc.vector.tensor_copy(
-                    out=grouped[:].rearrange("p (c i) j -> p c j i", i=4),
-                    in_=planes[:].rearrange("p j (c i) -> p c j i", i=4),
-                )
+                if s % 2 == 0:
+                    nc.vector.tensor_copy(
+                        out=grouped[:].rearrange("p (c i) j -> p c j i", i=4),
+                        in_=planes[:].rearrange("p j (c i) -> p c j i", i=4),
+                    )
+                else:
+                    nc.scalar.copy(
+                        out=grouped[:].rearrange("p (c i) j -> p c j i", i=4),
+                        in_=planes[:].rearrange("p j (c i) -> p c j i", i=4),
+                    )
                 nc.vector.quantize_mx(
                     out=codes[:, s, :].bitcast(FP8X4),
                     scales=scales[:, s, :],
@@ -262,5 +269,5 @@ def tile_multiheadselfattention_pa_kernel(
                         stop=(s == PASSES - 1),
                     )
                 scaled = out_pool.tile([P, T], F32)
-                nc.vector.tensor_scalar_mul(out=scaled[:], in0=acc[:], scalar1=1.0 / math.sqrt(K))
+                nc.scalar.mul(out=scaled[:], in_=acc[:], mul=1.0 / math.sqrt(K))
                 nc.sync.dma_start(out=out[0, h, frames, :], in_=scaled[:])

@@ -203,15 +203,26 @@ def tile_multiheadselfattention_pa_kernel(
             )
             rstd = stat_pool.tile([P, FRAME_TILES], F32)
             nc.gpsimd.tensor_tensor(out=rstd[:], in0=var_eps[:], in1=minus_half[:], op=ALU.pow)
+            offset = stat_pool.tile([P, FRAME_TILES], F32)
+            nc.gpsimd.tensor_tensor(out=offset[:], in0=neg_mean[:], in1=rstd[:], op=ALU.mult)
             for tt in range(FRAME_TILES):
-                nc.gpsimd.tensor_scalar(
-                    out=feat[:, tt, :],
-                    in0=feat[:, tt, :],
-                    scalar1=neg_mean[:, tt : tt + 1],
-                    scalar2=rstd[:, tt : tt + 1],
-                    op0=ALU.add,
-                    op1=ALU.mult,
-                )
+                if tt < FRAME_TILES - 1:
+                    nc.scalar.activation(
+                        out=feat[:, tt, :],
+                        in_=feat[:, tt, :],
+                        func=ACT.Identity,
+                        bias=offset[:, tt : tt + 1],
+                        scale=rstd[:, tt : tt + 1],
+                    )
+                else:
+                    nc.vector.tensor_scalar(
+                        out=feat[:, tt, :],
+                        in0=feat[:, tt, :],
+                        scalar1=neg_mean[:, tt : tt + 1],
+                        scalar2=rstd[:, tt : tt + 1],
+                        op0=ALU.add,
+                        op1=ALU.mult,
+                    )
 
             codes = code_pool.tile([P, PASSES, T], U32, align_bytes=64)
             scales = code_pool.tile([P, PASSES, T], U8, align_bytes=64)
@@ -235,16 +246,10 @@ def tile_multiheadselfattention_pa_kernel(
                         scale=gain_T[:, g, col : col + 1],
                     )
                 grouped = work_pool.tile([P, T, PACK], BF16, align_bytes=64)
-                if s % 2 == 0:
-                    nc.vector.tensor_copy(
-                        out=grouped[:].rearrange("p (c i) j -> p c j i", i=4),
-                        in_=planes[:].rearrange("p j (c i) -> p c j i", i=4),
-                    )
-                else:
-                    nc.scalar.copy(
-                        out=grouped[:].rearrange("p (c i) j -> p c j i", i=4),
-                        in_=planes[:].rearrange("p j (c i) -> p c j i", i=4),
-                    )
+                nc.vector.tensor_copy(
+                    out=grouped[:].rearrange("p (c i) j -> p c j i", i=4),
+                    in_=planes[:].rearrange("p j (c i) -> p c j i", i=4),
+                )
                 nc.vector.quantize_mx(
                     out=codes[:, s, :].bitcast(FP8X4),
                     scales=scales[:, s, :],

@@ -81,16 +81,14 @@ def tile_multiheadselfattention_pa_kernel(
             op=ALU.mult,
         )
 
-        x_pairs = const.tile([P, (F // 2) * T * 2], BF16)
-        x_words = x_pairs[:].bitcast(F32).rearrange("c (w t) -> c w t", t=T)
-        x_cols = x_pairs[:].rearrange("c (w t e) -> c w t e", t=T, e=2)
+        x_ft = const.tile([P, F, T], BF16)
         for tt in range(FRAME_TILES):
             frames = slice(tt * P, (tt + 1) * P)
-            x_raw = raw_pool.tile([P, P * F], BF16)
-            nc.sync.dma_start(out=x_raw[:], in_=x[0, :, frames, :].rearrange("c t f -> c (t f)"))
+            x_raw = raw_pool.tile([P, P, F], BF16)
+            nc.sync.dma_start(out=x_raw[:], in_=x[0, :, frames, :])
             nc.vector.tensor_copy(
-                out=x_words[:, :, frames],
-                in_=x_raw[:].bitcast(F32).rearrange("c (t w) -> c w t", w=F // 2),
+                out=x_ft[:, :, frames].rearrange("c (q i) t -> c q t i", i=4),
+                in_=x_raw[:].rearrange("c t (q i) -> c q t i", i=4),
             )
 
         bias_q = const.tile([P, H, D], BF16)
@@ -159,7 +157,7 @@ def tile_multiheadselfattention_pa_kernel(
                         f = j * OCT + f8
                         nc.tensor.matmul(
                             out=conv[:, f8, :],
-                            lhsT=x_cols[:, f // 2, frames, f % 2],
+                            lhsT=x_ft[:, f, frames],
                             rhs=w_T[:, g, :],
                             start=True,
                             stop=True,

@@ -40,7 +40,7 @@ def tile_multiheadselfattention_pa_kernel(
         feat_pool = ctx.enter_context(tc.tile_pool(name="feat", bufs=3))
         stat_pool = ctx.enter_context(tc.tile_pool(name="stat", bufs=4))
         work_pool = ctx.enter_context(tc.tile_pool(name="work", bufs=2))
-        code_pool = ctx.enter_context(tc.tile_pool(name="code", bufs=4))
+        code_pool = ctx.enter_context(tc.tile_pool(name="code", bufs=3))
         out_pool = ctx.enter_context(tc.tile_pool(name="outp", bufs=3))
         conv_psum = ctx.enter_context(tc.psum_pool(name="convp", bufs=3))
         turn_psum = ctx.enter_context(tc.psum_pool(name="turnp", bufs=3))
@@ -86,10 +86,16 @@ def tile_multiheadselfattention_pa_kernel(
             frames = slice(tt * P, (tt + 1) * P)
             x_raw = raw_pool.tile([P, P, F], BF16)
             nc.sync.dma_start(out=x_raw[:], in_=x[0, :, frames, :])
-            nc.vector.tensor_copy(
-                out=x_ft[:, :, frames].rearrange("c (q i) t -> c q t i", i=4),
-                in_=x_raw[:].rearrange("c t (q i) -> c q t i", i=4),
-            )
+            if tt == 0:
+                nc.vector.tensor_copy(
+                    out=x_ft[:, :, frames].rearrange("c (q i) t -> c q t i", i=4),
+                    in_=x_raw[:].rearrange("c t (q i) -> c q t i", i=4),
+                )
+            else:
+                nc.scalar.copy(
+                    out=x_ft[:, :, frames].rearrange("c (q i) t -> c q t i", i=4),
+                    in_=x_raw[:].rearrange("c t (q i) -> c q t i", i=4),
+                )
 
         bias_q = const.tile([P, H, D], BF16)
         nc.scalar.dma_start(
@@ -146,18 +152,19 @@ def tile_multiheadselfattention_pa_kernel(
             out=shift_T[:], in_=table_turned[:, 1, :].rearrange("p (g c) -> p g c", g=G)
         )
 
-        def quantised_features(g):
+        def quantised_features(g, vector_is_free):
             feat = feat_pool.tile([P, FRAME_TILES, K], F32)
             total = stat_pool.tile([P, FRAME_TILES], F32)
-            for tt in range(FRAME_TILES):
+            sq_total = stat_pool.tile([P, FRAME_TILES], F32)
+
+            def convolve(tt):
                 frames = slice(tt * P, (tt + 1) * P)
                 for j in range(PACK):
                     conv = conv_psum.tile([P, OCT, D], F32)
                     for f8 in range(OCT):
-                        f = j * OCT + f8
                         nc.tensor.matmul(
                             out=conv[:, f8, :],
-                            lhsT=x_ft[:, f, frames],
+                            lhsT=x_ft[:, j * OCT + f8, frames],
                             rhs=w_T[:, g, :],
                             start=True,
                             stop=True,
@@ -170,6 +177,8 @@ def tile_multiheadselfattention_pa_kernel(
                         in1=bias[:, g, :].unsqueeze(2).to_broadcast([P, D, OCT]),
                         op=ALU.add,
                     )
+
+            def prelu_and_squares(tt):
                 nc.vector.scalar_tensor_tensor(
                     out=feat[:, tt, :],
                     in0=feat[:, tt, :],
@@ -179,9 +188,6 @@ def tile_multiheadselfattention_pa_kernel(
                     op1=ALU.max,
                     accum_out=total[:, tt : tt + 1],
                 )
-
-            sq_total = stat_pool.tile([P, FRAME_TILES], F32)
-            for tt in range(FRAME_TILES):
                 squares = work_pool.tile([P, K], BF16)
                 nc.scalar.activation(
                     out=squares[:],
@@ -191,6 +197,13 @@ def tile_multiheadselfattention_pa_kernel(
                     scale=-1.0 * K,
                     accum_out=sq_total[:, tt : tt + 1],
                 )
+
+            for tt in range(FRAME_TILES):
+                convolve(tt)
+                if tt > 0:
+                    prelu_and_squares(tt - 1)
+            prelu_and_squares(FRAME_TILES - 1)
+
             neg_mean = stat_pool.tile([P, FRAME_TILES], F32)
             nc.gpsimd.tensor_scalar(
                 out=neg_mean[:], in0=total[:], scalar1=-1.0 / K, scalar2=0.0, op0=ALU.mult, op1=ALU.add
@@ -204,15 +217,7 @@ def tile_multiheadselfattention_pa_kernel(
             offset = stat_pool.tile([P, FRAME_TILES], F32)
             nc.gpsimd.tensor_tensor(out=offset[:], in0=neg_mean[:], in1=rstd[:], op=ALU.mult)
             for tt in range(FRAME_TILES):
-                if tt < FRAME_TILES - 1:
-                    nc.scalar.activation(
-                        out=feat[:, tt, :],
-                        in_=feat[:, tt, :],
-                        func=ACT.Identity,
-                        bias=offset[:, tt : tt + 1],
-                        scale=rstd[:, tt : tt + 1],
-                    )
-                else:
+                if tt == FRAME_TILES - 1 or (vector_is_free and tt % 2 == 1):
                     nc.vector.tensor_scalar(
                         out=feat[:, tt, :],
                         in0=feat[:, tt, :],
@@ -221,43 +226,65 @@ def tile_multiheadselfattention_pa_kernel(
                         op0=ALU.add,
                         op1=ALU.mult,
                     )
+                else:
+                    nc.scalar.activation(
+                        out=feat[:, tt, :],
+                        in_=feat[:, tt, :],
+                        func=ACT.Identity,
+                        bias=offset[:, tt : tt + 1],
+                        scale=rstd[:, tt : tt + 1],
+                    )
 
             codes = code_pool.tile([P, PASSES, T], U32, align_bytes=64)
             scales = code_pool.tile([P, PASSES, T], U8, align_bytes=64)
-            for s in range(PASSES):
-                planes = work_pool.tile([P, PACK, T], BF16)
-                for j in range(PACK):
-                    turned = turn_psum.tile([P, T], F32)
-                    first = j * K_PASS + s * P
-                    for tt in range(FRAME_TILES):
-                        nc.tensor.transpose(
-                            turned[:, tt * P : (tt + 1) * P],
-                            feat[:, tt, first : first + P],
-                            ident_f32[:],
-                        )
-                    col = s * PACK + j
-                    nc.scalar.activation(
-                        out=planes[:, j, :],
-                        in_=turned[:],
-                        func=ACT.Identity,
-                        bias=shift_T[:, g, col : col + 1],
-                        scale=gain_T[:, g, col : col + 1],
+            for half in range(PASSES // 2):
+                grouped = work_pool.tile([P, 2, T, PACK], BF16, align_bytes=64)
+                for s2 in range(2):
+                    s = 2 * half + s2
+                    planes = work_pool.tile([P, PACK, T], BF16)
+                    for j in range(PACK):
+                        turned = turn_psum.tile([P, T], F32)
+                        first = j * K_PASS + s * P
+                        for tt in range(FRAME_TILES):
+                            nc.tensor.transpose(
+                                turned[:, tt * P : (tt + 1) * P],
+                                feat[:, tt, first : first + P],
+                                ident_f32[:],
+                            )
+                        col = s * PACK + j
+                        if vector_is_free and j % 2 == 1:
+                            nc.vector.tensor_scalar(
+                                out=planes[:, j, :],
+                                in0=turned[:],
+                                scalar1=gain_T[:, g, col : col + 1],
+                                scalar2=shift_T[:, g, col : col + 1],
+                                op0=ALU.mult,
+                                op1=ALU.add,
+                            )
+                        else:
+                            nc.scalar.activation(
+                                out=planes[:, j, :],
+                                in_=turned[:],
+                                func=ACT.Identity,
+                                bias=shift_T[:, g, col : col + 1],
+                                scale=gain_T[:, g, col : col + 1],
+                            )
+                    nc.vector.tensor_copy(
+                        out=grouped[:, s2, :, :].rearrange("p (c i) j -> p c j i", i=4),
+                        in_=planes[:].rearrange("p j (c i) -> p c j i", i=4),
                     )
-                grouped = work_pool.tile([P, T, PACK], BF16, align_bytes=64)
-                nc.vector.tensor_copy(
-                    out=grouped[:].rearrange("p (c i) j -> p c j i", i=4),
-                    in_=planes[:].rearrange("p j (c i) -> p c j i", i=4),
-                )
                 nc.vector.quantize_mx(
-                    out=codes[:, s, :].bitcast(FP8X4),
-                    scales=scales[:, s, :],
-                    in_=grouped[:].rearrange("p t j -> p (t j)"),
+                    out=codes[:, 2 * half : 2 * half + 2, :]
+                    .rearrange("p s t -> p (s t)")
+                    .bitcast(FP8X4),
+                    scales=scales[:, 2 * half : 2 * half + 2, :].rearrange("p s t -> p (s t)"),
+                    in_=grouped[:].rearrange("p s t j -> p (s t j)"),
                 )
             return codes, scales
 
         for h in range(H):
-            q_codes, q_scales = quantised_features(h)
-            k_codes, k_scales = quantised_features(H + h)
+            q_codes, q_scales = quantised_features(h, False)
+            k_codes, k_scales = quantised_features(H + h, h == H - 1)
             for tt in range(FRAME_TILES):
                 frames = slice(tt * P, (tt + 1) * P)
                 acc = score_psum.tile([P, T], F32)

@@ -42,9 +42,8 @@ def tile_multiheadselfattention_pa_kernel(
         work_pool = ctx.enter_context(tc.tile_pool(name="work", bufs=2))
         code_pool = ctx.enter_context(tc.tile_pool(name="code", bufs=3))
         out_pool = ctx.enter_context(tc.tile_pool(name="outp", bufs=3))
-        conv_psum = ctx.enter_context(tc.psum_pool(name="convp", bufs=3))
-        turn_psum = ctx.enter_context(tc.psum_pool(name="turnp", bufs=3))
-        score_psum = ctx.enter_context(tc.psum_pool(name="scorep", bufs=2))
+        conv_psum = ctx.enter_context(tc.psum_pool(name="convp", bufs=4))
+        turn_psum = ctx.enter_context(tc.psum_pool(name="turnp", bufs=4))
 
         ident_f32 = const.tile([P, P], F32)
         make_identity(nc, ident_f32[:])
@@ -287,7 +286,7 @@ def tile_multiheadselfattention_pa_kernel(
             k_codes, k_scales = quantised_features(H + h, h == H - 1)
             for tt in range(FRAME_TILES):
                 frames = slice(tt * P, (tt + 1) * P)
-                acc = score_psum.tile([P, T], F32)
+                acc = turn_psum.tile([P, T], F32, tag="turned")
                 for s in range(PASSES):
                     nc.tensor.matmul_mx(
                         out=acc[:],

@@ -240,7 +240,7 @@ def tile_multiheadselfattention_pa_kernel(
                 grouped = work_pool.tile([P, 2, T, PACK], BF16, align_bytes=64)
                 for s2 in range(2):
                     s = 2 * half + s2
-                    planes = work_pool.tile([P, PACK, T], BF16)
+                    planes = work_pool.tile([P, PACK, T], BF16, bufs=4)
                     for j in range(PACK):
                         turned = turn_psum.tile([P, T], F32)
                         first = j * K_PASS + s * P

@@ -26,6 +26,12 @@ PACK = 4
 K_PASS = P * PACK
 PASSES = K // K_PASS
 OCT = F // PACK
+UNITS = G * FRAME_TILES
+LAG_TURN = 7
+LAG_STAT = 2
+FEAT_BUFS = 12
+SPLIT = 352
+SPLIT_END = 160
 
 FLOPS = 2 * C * (G * D) * (T * F) + 2 * H * T * T * K
 
@@ -37,8 +43,8 @@ def tile_multiheadselfattention_pa_kernel(
     with ExitStack() as ctx:
         const = ctx.enter_context(tc.tile_pool(name="const", bufs=1))
         raw_pool = ctx.enter_context(tc.tile_pool(name="raw", bufs=2))
-        feat_pool = ctx.enter_context(tc.tile_pool(name="feat", bufs=3))
-        stat_pool = ctx.enter_context(tc.tile_pool(name="stat", bufs=4))
+        feat_pool = ctx.enter_context(tc.tile_pool(name="feat", bufs=FEAT_BUFS))
+        stat_pool = ctx.enter_context(tc.tile_pool(name="stat", bufs=8))
         work_pool = ctx.enter_context(tc.tile_pool(name="work", bufs=2))
         code_pool = ctx.enter_context(tc.tile_pool(name="code", bufs=3))
         out_pool = ctx.enter_context(tc.tile_pool(name="outp", bufs=3))
@@ -49,8 +55,11 @@ def tile_multiheadselfattention_pa_kernel(
         make_identity(nc, ident_f32[:])
         ident_bf = const.tile([P, P], BF16)
         make_identity(nc, ident_bf[:])
-        minus_half = const.tile([P, FRAME_TILES], F32)
-        nc.vector.memset(minus_half[:], -0.5)
+
+        zero_col = const.tile([P, 1], F32)
+        nc.vector.memset(zero_col[:], 0.0)
+        eps_col = const.tile([P, 1], F32)
+        nc.vector.tensor_scalar_add(out=eps_col[:], in0=zero_col[:], scalar1=EPS)
 
         slope_q = const.tile([P, H], BF16)
         nc.scalar.dma_start(out=slope_q[:], in_=aq.partition_broadcast(P))
@@ -151,152 +160,223 @@ def tile_multiheadselfattention_pa_kernel(
             out=shift_T[:], in_=table_turned[:, 1, :].rearrange("p (g c) -> p g c", g=G)
         )
 
-        def quantised_features(g, vector_is_free):
-            feat = feat_pool.tile([P, FRAME_TILES, K], F32)
-            total = stat_pool.tile([P, FRAME_TILES], F32)
-            sq_total = stat_pool.tile([P, FRAME_TILES], F32)
+        feat = {}
+        total = {}
+        sq_total = {}
+        rstd = {}
+        offset = {}
+        planes = {}
+        grouped = {}
+        codes = {}
+        scales = {}
 
-            def convolve(tt):
-                frames = slice(tt * P, (tt + 1) * P)
-                for j in range(PACK):
-                    conv = conv_psum.tile([P, OCT, D], F32)
-                    for f8 in range(OCT):
-                        nc.tensor.matmul(
-                            out=conv[:, f8, :],
-                            lhsT=x_ft[:, j * OCT + f8, frames],
-                            rhs=w_T[:, g, :],
-                            start=True,
-                            stop=True,
-                        )
-                    nc.vector.tensor_tensor(
-                        out=feat[:, tt, j * K_PASS : (j + 1) * K_PASS].rearrange(
-                            "p (d f) -> p d f", f=OCT
-                        ),
-                        in0=conv[:].rearrange("p f d -> p d f"),
-                        in1=bias[:, g, :].unsqueeze(2).to_broadcast([P, D, OCT]),
-                        op=ALU.add,
+        def group_of(u):
+            i = u // FRAME_TILES
+            return (i % 2) * H + i // 2
+
+        def convolve(u):
+            g, tt = group_of(u), u % FRAME_TILES
+            frames = slice(tt * P, (tt + 1) * P)
+            banks = []
+            for j in range(PACK):
+                conv = conv_psum.tile([P, OCT, D], F32)
+                for f8 in range(OCT):
+                    nc.tensor.matmul(
+                        out=conv[:, f8, :],
+                        lhsT=x_ft[:, j * OCT + f8, frames],
+                        rhs=w_T[:, g, :],
+                        start=True,
+                        stop=True,
                     )
+                banks.append(conv)
+            return banks
 
-            def prelu_and_squares(tt):
-                nc.vector.scalar_tensor_tensor(
-                    out=feat[:, tt, :],
-                    in0=feat[:, tt, :],
-                    scalar=slope[:, g : g + 1],
-                    in1=feat[:, tt, :],
+        def add_bias(u, banks):
+            g = group_of(u)
+            feat_u = feat_pool.tile([P, K], F32)
+            feat[u] = feat_u
+            for j in range(PACK):
+                nc.vector.tensor_tensor(
+                    out=feat_u[:, j * K_PASS : (j + 1) * K_PASS].rearrange("p (d f) -> p d f", f=OCT),
+                    in0=banks[j][:].rearrange("p f d -> p d f"),
+                    in1=bias[:, g, :].unsqueeze(2).to_broadcast([P, D, OCT]),
+                    op=ALU.add,
+                )
+
+        def prelu(u):
+            g = group_of(u)
+            total_u = stat_pool.tile([P, 1], F32)
+            total[u] = total_u
+            nc.vector.scalar_tensor_tensor(
+                out=feat[u][:],
+                in0=feat[u][:],
+                scalar=slope[:, g : g + 1],
+                in1=feat[u][:],
+                op0=ALU.mult,
+                op1=ALU.max,
+                accum_out=total_u[:],
+            )
+
+        def squares(u):
+            sq_u = stat_pool.tile([P, 1], F32)
+            sq_total[u] = sq_u
+            junk = work_pool.tile([P, K], BF16, bufs=1)
+            nc.scalar.activation(
+                out=junk[:],
+                in_=feat[u][:],
+                func=ACT.Square,
+                bias=total[u][:],
+                scale=-1.0 * K,
+                accum_out=sq_u[:],
+            )
+
+        def inverse_deviation(u):
+            rstd_u = stat_pool.tile([P, 1], F32)
+            rstd[u] = rstd_u
+            nc.scalar.activation(
+                out=rstd_u[:],
+                in_=sq_total[u][:],
+                func=ACT.Abs_reciprocal_sqrt,
+                bias=eps_col[:],
+                scale=1.0 / (K * K * K),
+            )
+
+        def release(u):
+            offset_u = stat_pool.tile([P, 1], F32)
+            offset[u] = offset_u
+            nc.vector.tensor_scalar(
+                out=offset_u[:],
+                in0=total[u][:],
+                scalar1=rstd[u][:],
+                scalar2=-1.0 / K,
+                op0=ALU.mult,
+                op1=ALU.mult,
+            )
+
+        def normalise(u, engine):
+            engine.tensor_scalar(
+                out=feat[u][:],
+                in0=feat[u][:],
+                scalar1=rstd[u][:],
+                scalar2=offset[u][:],
+                op0=ALU.mult,
+                op1=ALU.add,
+            )
+
+        def turn(b):
+            i, s = b // PASSES, b % PASSES
+            banks = []
+            for j in range(PACK):
+                turned = turn_psum.tile([P, T], F32)
+                first = j * K_PASS + s * P
+                for tt in range(FRAME_TILES):
+                    nc.tensor.transpose(
+                        turned[:, tt * P : (tt + 1) * P],
+                        feat[i * FRAME_TILES + tt][:, first : first + P],
+                        ident_f32[:],
+                    )
+                banks.append(turned)
+            return banks
+
+        def gain_shift(b, j, turned, on_vector):
+            g, s = group_of(b), b % PASSES
+            col = s * PACK + j
+            if on_vector:
+                nc.vector.tensor_scalar(
+                    out=planes[b][:, j, :],
+                    in0=turned[:],
+                    scalar1=gain_T[:, g, col : col + 1],
+                    scalar2=shift_T[:, g, col : col + 1],
                     op0=ALU.mult,
-                    op1=ALU.max,
-                    accum_out=total[:, tt : tt + 1],
+                    op1=ALU.add,
                 )
-                squares = work_pool.tile([P, K], BF16)
+            else:
                 nc.scalar.activation(
-                    out=squares[:],
-                    in_=feat[:, tt, :],
-                    func=ACT.Square,
-                    bias=total[:, tt : tt + 1],
-                    scale=-1.0 * K,
-                    accum_out=sq_total[:, tt : tt + 1],
+                    out=planes[b][:, j, :],
+                    in_=turned[:],
+                    func=ACT.Identity,
+                    bias=shift_T[:, g, col : col + 1],
+                    scale=gain_T[:, g, col : col + 1],
                 )
 
-            for tt in range(FRAME_TILES):
-                convolve(tt)
-                if tt > 0:
-                    prelu_and_squares(tt - 1)
-            prelu_and_squares(FRAME_TILES - 1)
-
-            neg_mean = stat_pool.tile([P, FRAME_TILES], F32)
-            nc.gpsimd.tensor_scalar(
-                out=neg_mean[:], in0=total[:], scalar1=-1.0 / K, scalar2=0.0, op0=ALU.mult, op1=ALU.add
+        def regroup(b, split):
+            if b % 2 == 0:
+                pair = work_pool.tile([P, 2, T, PACK], BF16, align_bytes=64)
+                grouped[b // 2] = pair
+            pair = grouped[b // 2]
+            nc.scalar.copy(
+                out=pair[:, b % 2, 0:split, :].rearrange("p (c i) j -> p c j i", i=4),
+                in_=planes[b][:, :, 0:split].rearrange("p j (c i) -> p c j i", i=4),
             )
-            var_eps = stat_pool.tile([P, FRAME_TILES], F32)
-            nc.gpsimd.tensor_scalar(
-                out=var_eps[:], in0=sq_total[:], scalar1=1.0 / (K * K * K), scalar2=EPS, op0=ALU.mult, op1=ALU.add
+            nc.vector.tensor_copy(
+                out=pair[:, b % 2, split:T, :].rearrange("p (c i) j -> p c j i", i=4),
+                in_=planes[b][:, :, split:T].rearrange("p j (c i) -> p c j i", i=4),
             )
-            rstd = stat_pool.tile([P, FRAME_TILES], F32)
-            nc.gpsimd.tensor_tensor(out=rstd[:], in0=var_eps[:], in1=minus_half[:], op=ALU.pow)
-            offset = stat_pool.tile([P, FRAME_TILES], F32)
-            nc.gpsimd.tensor_tensor(out=offset[:], in0=neg_mean[:], in1=rstd[:], op=ALU.mult)
-            for tt in range(FRAME_TILES):
-                if tt == FRAME_TILES - 1 or (vector_is_free and tt % 2 == 1):
-                    nc.vector.tensor_scalar(
-                        out=feat[:, tt, :],
-                        in0=feat[:, tt, :],
-                        scalar1=neg_mean[:, tt : tt + 1],
-                        scalar2=rstd[:, tt : tt + 1],
-                        op0=ALU.add,
-                        op1=ALU.mult,
-                    )
-                else:
-                    nc.scalar.activation(
-                        out=feat[:, tt, :],
-                        in_=feat[:, tt, :],
-                        func=ACT.Identity,
-                        bias=offset[:, tt : tt + 1],
-                        scale=rstd[:, tt : tt + 1],
-                    )
 
-            codes = code_pool.tile([P, PASSES, T], U32, align_bytes=64)
-            scales = code_pool.tile([P, PASSES, T], U8, align_bytes=64)
-            for half in range(PASSES // 2):
-                grouped = work_pool.tile([P, 2, T, PACK], BF16, align_bytes=64)
-                for s2 in range(2):
-                    s = 2 * half + s2
-                    planes = work_pool.tile([P, PACK, T], BF16, bufs=4)
-                    for j in range(PACK):
-                        turned = turn_psum.tile([P, T], F32)
-                        first = j * K_PASS + s * P
-                        for tt in range(FRAME_TILES):
-                            nc.tensor.transpose(
-                                turned[:, tt * P : (tt + 1) * P],
-                                feat[:, tt, first : first + P],
-                                ident_f32[:],
-                            )
-                        col = s * PACK + j
-                        if vector_is_free and j % 2 == 1:
-                            nc.vector.tensor_scalar(
-                                out=planes[:, j, :],
-                                in0=turned[:],
-                                scalar1=gain_T[:, g, col : col + 1],
-                                scalar2=shift_T[:, g, col : col + 1],
-                                op0=ALU.mult,
-                                op1=ALU.add,
-                            )
-                        else:
-                            nc.scalar.activation(
-                                out=planes[:, j, :],
-                                in_=turned[:],
-                                func=ACT.Identity,
-                                bias=shift_T[:, g, col : col + 1],
-                                scale=gain_T[:, g, col : col + 1],
-                            )
-                    nc.vector.tensor_copy(
-                        out=grouped[:, s2, :, :].rearrange("p (c i) j -> p c j i", i=4),
-                        in_=planes[:].rearrange("p j (c i) -> p c j i", i=4),
-                    )
-                nc.vector.quantize_mx(
-                    out=codes[:, 2 * half : 2 * half + 2, :]
-                    .rearrange("p s t -> p (s t)")
-                    .bitcast(FP8X4),
-                    scales=scales[:, 2 * half : 2 * half + 2, :].rearrange("p s t -> p (s t)"),
-                    in_=grouped[:].rearrange("p s t j -> p (s t j)"),
+        def quantise(pair_no):
+            i, half = pair_no // 2, pair_no % 2
+            if half == 0:
+                codes_i = code_pool.tile([P, PASSES, T], U32, align_bytes=64)
+                scales_i = code_pool.tile([P, PASSES, T], U8, align_bytes=64)
+                codes[i] = codes_i
+                scales[i] = scales_i
+            nc.vector.quantize_mx(
+                out=codes[i][:, 2 * half : 2 * half + 2, :].rearrange("p s t -> p (s t)").bitcast(FP8X4),
+                scales=scales[i][:, 2 * half : 2 * half + 2, :].rearrange("p s t -> p (s t)"),
+                in_=grouped[pair_no][:].rearrange("p s t j -> p (s t j)"),
+            )
+
+        def scores(h, tt, on_vector):
+            frames = slice(tt * P, (tt + 1) * P)
+            acc = turn_psum.tile([P, T], F32, tag="turned")
+            for s in range(PASSES):
+                nc.tensor.matmul_mx(
+                    out=acc[:],
+                    lhsT=codes[2 * h][:, s, frames].bitcast(FP8X4),
+                    lhsT_scale=scales[2 * h][:, s, frames],
+                    rhs=codes[2 * h + 1][:, s, :].bitcast(FP8X4),
+                    rhs_scale=scales[2 * h + 1][:, s, :],
+                    start=(s == 0),
+                    stop=(s == PASSES - 1),
                 )
-            return codes, scales
-
-        for h in range(H):
-            q_codes, q_scales = quantised_features(h, False)
-            k_codes, k_scales = quantised_features(H + h, h == H - 1)
-            for tt in range(FRAME_TILES):
-                frames = slice(tt * P, (tt + 1) * P)
-                acc = turn_psum.tile([P, T], F32, tag="turned")
-                for s in range(PASSES):
-                    nc.tensor.matmul_mx(
-                        out=acc[:],
-                        lhsT=q_codes[:, s, frames].bitcast(FP8X4),
-                        lhsT_scale=q_scales[:, s, frames],
-                        rhs=k_codes[:, s, :].bitcast(FP8X4),
-                        rhs_scale=k_scales[:, s, :],
-                        start=(s == 0),
-                        stop=(s == PASSES - 1),
-                    )
-                scaled = out_pool.tile([P, T], F32)
+            scaled = out_pool.tile([P, T], F32)
+            if on_vector:
+                nc.vector.tensor_scalar_mul(out=scaled[:], in0=acc[:], scalar1=1.0 / math.sqrt(K))
+            else:
                 nc.scalar.mul(out=scaled[:], in_=acc[:], mul=1.0 / math.sqrt(K))
-                nc.sync.dma_start(out=out[0, h, frames, :], in_=scaled[:])
+            nc.sync.dma_start(out=out[0, h, frames, :], in_=scaled[:])
+
+        with tc.manual_schedule():
+            for n in range(UNITS + LAG_TURN + 6):
+                b = n - LAG_TURN
+                vector_is_free = n > UNITS
+                u_norm = n - 1 - LAG_STAT
+                if 0 <= u_norm < UNITS:
+                    normalise(u_norm, nc.vector if n >= UNITS else nc.gpsimd)
+                conv_banks = convolve(n) if n < UNITS else None
+                if 0 <= n - 1 < UNITS:
+                    squares(n - 1)
+                if n < UNITS:
+                    add_bias(n, conv_banks)
+                if 0 <= b < UNITS:
+                    planes_b = work_pool.tile([P, PACK, T], BF16, bufs=3)
+                    planes[b] = planes_b
+                    turned_banks = turn(b)
+                    gain_shift(b, 0, turned_banks[0], False)
+                if 0 <= n - 1 < UNITS:
+                    inverse_deviation(n - 1)
+                if 0 <= b < UNITS:
+                    gain_shift(b, 1, turned_banks[1], vector_is_free)
+                    gain_shift(b, 2, turned_banks[2], False)
+                    gain_shift(b, 3, turned_banks[3], True)
+                if 0 <= b - 1 < UNITS:
+                    regroup(b - 1, SPLIT_END if vector_is_free else SPLIT)
+                if b % 2 == 1 and 0 <= b - 3 < UNITS:
+                    quantise((b - 3) // 2)
+                if 0 <= n - LAG_STAT < UNITS:
+                    release(n - LAG_STAT)
+                if n < UNITS:
+                    prelu(n)
+                r = b - 6
+                if 0 <= r < UNITS and (r // FRAME_TILES) % 2 == 1:
+                    scores(r // (2 * FRAME_TILES), r % FRAME_TILES, vector_is_free and r % 2 == 1)

@@ -42,12 +42,11 @@ def tile_multiheadselfattention_pa_kernel(
     nc = tc.nc
     with ExitStack() as ctx:
         const = ctx.enter_context(tc.tile_pool(name="const", bufs=1))
-        raw_pool = ctx.enter_context(tc.tile_pool(name="raw", bufs=2))
         feat_pool = ctx.enter_context(tc.tile_pool(name="feat", bufs=FEAT_BUFS))
         stat_pool = ctx.enter_context(tc.tile_pool(name="stat", bufs=8))
         work_pool = ctx.enter_context(tc.tile_pool(name="work", bufs=2))
         code_pool = ctx.enter_context(tc.tile_pool(name="code", bufs=3))
-        out_pool = ctx.enter_context(tc.tile_pool(name="outp", bufs=3))
+        out_pool = ctx.enter_context(tc.tile_pool(name="outp", bufs=FRAME_TILES))
         conv_psum = ctx.enter_context(tc.psum_pool(name="convp", bufs=4))
         turn_psum = ctx.enter_context(tc.psum_pool(name="turnp", bufs=4))
 
@@ -90,20 +89,11 @@ def tile_multiheadselfattention_pa_kernel(
         )
 
         x_ft = const.tile([P, F, T], BF16)
+        x_raw = []
         for tt in range(FRAME_TILES):
-            frames = slice(tt * P, (tt + 1) * P)
-            x_raw = raw_pool.tile([P, P, F], BF16)
-            nc.sync.dma_start(out=x_raw[:], in_=x[0, :, frames, :])
-            if tt == 0:
-                nc.vector.tensor_copy(
-                    out=x_ft[:, :, frames].rearrange("c (q i) t -> c q t i", i=4),
-                    in_=x_raw[:].rearrange("c t (q i) -> c q t i", i=4),
-                )
-            else:
-                nc.scalar.copy(
-                    out=x_ft[:, :, frames].rearrange("c (q i) t -> c q t i", i=4),
-                    in_=x_raw[:].rearrange("c t (q i) -> c q t i", i=4),
-                )
+            raw = feat_pool.tile([P, P, F], BF16, tag="feat_u")
+            nc.sync.dma_start(out=raw[:], in_=x[0, :, tt * P : (tt + 1) * P, :])
+            x_raw.append(raw)
 
         bias_q = const.tile([P, H, D], BF16)
         nc.scalar.dma_start(
@@ -135,30 +125,36 @@ def tile_multiheadselfattention_pa_kernel(
             for rows_bf, table in ((gain_rows_bf, lw), (shift_rows_bf, lb)):
                 by_j = table.rearrange("h (s d) (j f) -> j (h s) d f", s=PASSES, j=PACK)
                 for j in range(PACK):
-                    nc.scalar.dma_start(
+                    nc.sync.dma_start(
                         out=rows_bf[side * 64 + j : (side + 1) * 64 : PACK, :].rearrange(
                             "r (d f) -> r d f", f=OCT
                         ),
                         in_=by_j[j],
                     )
         gain_rows = const.tile([P, P], F32)
-        nc.vector.tensor_copy(out=gain_rows[:], in_=gain_rows_bf[:])
         shift_rows = const.tile([P, P], F32)
-        nc.vector.tensor_copy(out=shift_rows[:], in_=shift_rows_bf[:])
-        table_turned = turn_psum.tile([P, 2, P], F32, tag="turned")
-        nc.tensor.transpose(table_turned[:, 0, :], gain_rows[:], ident_f32[:])
-        nc.tensor.transpose(table_turned[:, 1, :], shift_rows[:], ident_f32[:])
         gain_T = const.tile([P, G, PASSES * PACK], F32)
-        nc.vector.tensor_tensor(
-            out=gain_T[:],
-            in0=table_turned[:, 0, :].rearrange("p (g c) -> p g c", g=G),
-            in1=sign[:].unsqueeze(2).to_broadcast([P, G, PASSES * PACK]),
-            op=ALU.mult,
-        )
         shift_T = const.tile([P, G, PASSES * PACK], F32)
-        nc.vector.tensor_copy(
-            out=shift_T[:], in_=table_turned[:, 1, :].rearrange("p (g c) -> p g c", g=G)
-        )
+        tables = []
+
+        def turn_tables():
+            nc.vector.tensor_copy(out=gain_rows[:], in_=gain_rows_bf[:])
+            nc.vector.tensor_copy(out=shift_rows[:], in_=shift_rows_bf[:])
+            table_turned = turn_psum.tile([P, 2, P], F32, tag="turned")
+            nc.tensor.transpose(table_turned[:, 0, :], gain_rows[:], ident_f32[:])
+            nc.tensor.transpose(table_turned[:, 1, :], shift_rows[:], ident_f32[:])
+            tables.append(table_turned)
+
+        def finish_tables():
+            nc.vector.tensor_tensor(
+                out=gain_T[:],
+                in0=tables[0][:, 0, :].rearrange("p (g c) -> p g c", g=G),
+                in1=sign[:].unsqueeze(2).to_broadcast([P, G, PASSES * PACK]),
+                op=ALU.mult,
+            )
+            nc.vector.tensor_copy(
+                out=shift_T[:], in_=tables[0][:, 1, :].rearrange("p (g c) -> p g c", g=G)
+            )
 
         feat = {}
         total = {}
@@ -174,6 +170,13 @@ def tile_multiheadselfattention_pa_kernel(
             i = u // FRAME_TILES
             return (i % 2) * H + i // 2
 
+        def copy_x(half):
+            tt, first = half // 2, (half % 2) * (F // 2)
+            nc.scalar.copy(
+                out=x_ft[:, first : first + F // 2, tt * P : (tt + 1) * P].rearrange("c (q i) t -> c q t i", i=4),
+                in_=x_raw[tt][:, :, first : first + F // 2].rearrange("c t (q i) -> c q t i", i=4),
+            )
+
         def convolve(u):
             g, tt = group_of(u), u % FRAME_TILES
             frames = slice(tt * P, (tt + 1) * P)
@@ -183,7 +186,7 @@ def tile_multiheadselfattention_pa_kernel(
                 for f8 in range(OCT):
                     nc.tensor.matmul(
                         out=conv[:, f8, :],
-                        lhsT=x_ft[:, j * OCT + f8, frames],
+                        lhsT=(x_raw[tt][:, :, j * OCT + f8] if u < FRAME_TILES else x_ft[:, j * OCT + f8, frames]),
                         rhs=w_T[:, g, :],
                         start=True,
                         stop=True,
@@ -326,10 +329,17 @@ def tile_multiheadselfattention_pa_kernel(
                 in_=grouped[pair_no][:].rearrange("p s t j -> p (s t j)"),
             )
 
-        def scores(h, tt, on_vector):
+        def quantise_pass(b):
+            i, s = b // PASSES, b % PASSES
+            nc.vector.quantize_mx(
+                out=codes[i][:, s, :].bitcast(FP8X4),
+                scales=scales[i][:, s, :],
+                in_=grouped[b // 2][:, b % 2, :, :].rearrange("p t j -> p (t j)"),
+            )
+
+        def score_passes(h, tt, acc, passes):
             frames = slice(tt * P, (tt + 1) * P)
-            acc = turn_psum.tile([P, T], F32, tag="turned")
-            for s in range(PASSES):
+            for s in passes:
                 nc.tensor.matmul_mx(
                     out=acc[:],
                     lhsT=codes[2 * h][:, s, frames].bitcast(FP8X4),
@@ -339,6 +349,9 @@ def tile_multiheadselfattention_pa_kernel(
                     start=(s == 0),
                     stop=(s == PASSES - 1),
                 )
+
+        def store_scores(h, tt, acc, on_vector):
+            frames = slice(tt * P, (tt + 1) * P)
             scaled = out_pool.tile([P, T], F32)
             if on_vector:
                 nc.vector.tensor_scalar_mul(out=scaled[:], in0=acc[:], scalar1=1.0 / math.sqrt(K))
@@ -346,8 +359,9 @@ def tile_multiheadselfattention_pa_kernel(
                 nc.scalar.mul(out=scaled[:], in_=acc[:], mul=1.0 / math.sqrt(K))
             nc.sync.dma_start(out=out[0, h, frames, :], in_=scaled[:])
 
+        last_acc = []
         with tc.manual_schedule():
-            for n in range(UNITS + LAG_TURN + 6):
+            for n in range(UNITS + LAG_TURN + 2):
                 b = n - LAG_TURN
                 vector_is_free = n > UNITS
                 u_norm = n - 1 - LAG_STAT
@@ -365,18 +379,41 @@ def tile_multiheadselfattention_pa_kernel(
                     gain_shift(b, 0, turned_banks[0], False)
                 if 0 <= n - 1 < UNITS:
                     inverse_deviation(n - 1)
+                if n == 0:
+                    copy_x(0)
+                if n + 1 < 2 * FRAME_TILES:
+                    copy_x(n + 1)
                 if 0 <= b < UNITS:
                     gain_shift(b, 1, turned_banks[1], vector_is_free)
                     gain_shift(b, 2, turned_banks[2], False)
                     gain_shift(b, 3, turned_banks[3], True)
                 if 0 <= b - 1 < UNITS:
                     regroup(b - 1, SPLIT_END if vector_is_free else SPLIT)
-                if b % 2 == 1 and 0 <= b - 3 < UNITS:
+                if b % 2 == 1 and 0 <= b - 3 < UNITS - 2:
                     quantise((b - 3) // 2)
+                if UNITS <= b:
+                    quantise_pass(b - 2)
+                if n == 2:
+                    turn_tables()
+                if n == 4:
+                    finish_tables()
                 if 0 <= n - LAG_STAT < UNITS:
                     release(n - LAG_STAT)
                 if n < UNITS:
                     prelu(n)
                 r = b - 6
-                if 0 <= r < UNITS and (r // FRAME_TILES) % 2 == 1:
-                    scores(r // (2 * FRAME_TILES), r % FRAME_TILES, vector_is_free and r % 2 == 1)
+                if 0 <= r < UNITS - FRAME_TILES and (r // FRAME_TILES) % 2 == 1:
+                    acc = turn_psum.tile([P, T], F32, tag="turned")
+                    score_passes(r // (2 * FRAME_TILES), r % FRAME_TILES, acc, range(PASSES))
+                    store_scores(r // (2 * FRAME_TILES), r % FRAME_TILES, acc, vector_is_free and r % 2 == 1)
+                if b == UNITS - 1:
+                    for tt in range(FRAME_TILES):
+                        acc = conv_psum.tile([P, T], F32, tag="conv")
+                        last_acc.append(acc)
+                        score_passes(H - 1, tt, acc, (0, 1))
+                if UNITS <= b:
+                    for tt in range(FRAME_TILES):
+                        score_passes(H - 1, tt, last_acc[tt], (b - UNITS + 2,))
+                if b == UNITS + 1:
+                    for tt in range(FRAME_TILES):
+                        store_scores(H - 1, tt, last_acc[tt], tt % 2 == 1)

@@ -31,7 +31,7 @@ LAG_TURN = 7
 LAG_STAT = 2
 FEAT_BUFS = 12
 SPLIT = 352
-SPLIT_END = 160
+SPLIT_END = 256
 
 FLOPS = 2 * C * (G * D) * (T * F) + 2 * H * T * T * K
 
@@ -403,7 +403,10 @@ def tile_multiheadselfattention_pa_kernel(
                     prelu(n)
                 r = b - 6
                 if 0 <= r < UNITS - FRAME_TILES and (r // FRAME_TILES) % 2 == 1:
-                    acc = turn_psum.tile([P, T], F32, tag="turned")
+                    if n < UNITS:
+                        acc = turn_psum.tile([P, T], F32, tag="turned")
+                    else:
+                        acc = conv_psum.tile([P, T], F32, tag="conv")
                     score_passes(r // (2 * FRAME_TILES), r % FRAME_TILES, acc, range(PASSES))
                     store_scores(r // (2 * FRAME_TILES), r % FRAME_TILES, acc, vector_is_free and r % 2 == 1)
                 if b == UNITS - 1:

@@ -27,10 +27,10 @@ K_PASS = P * PACK
 PASSES = K // K_PASS
 OCT = F // PACK
 UNITS = G * FRAME_TILES
-LAG_TURN = 7
-LAG_STAT = 2
+LAG_TURN = 6
+LAG_STAT = 1
 FEAT_BUFS = 12
-SPLIT = 352
+SPLIT = 416
 SPLIT_END = 256
 
 FLOPS = 2 * C * (G * D) * (T * F) + 2 * H * T * T * K
@@ -95,29 +95,19 @@ def tile_multiheadselfattention_pa_kernel(
             nc.sync.dma_start(out=raw[:], in_=x[0, :, tt * P : (tt + 1) * P, :])
             x_raw.append(raw)
 
-        bias_q = const.tile([P, H, D], BF16)
-        nc.scalar.dma_start(
-            out=bias_q[:].rearrange("p h d -> p (h d)"),
-            in_=bq.rearrange("h d -> (h d)").partition_broadcast(P),
-        )
-        bias_k = const.tile([P, H, D], BF16)
-        nc.scalar.dma_start(
-            out=bias_k[:].rearrange("p h d -> p (h d)"),
-            in_=bk.rearrange("h d -> (h d)").partition_broadcast(P),
-        )
-        bias = const.tile([P, G, D], F32)
-        nc.vector.tensor_tensor(
-            out=bias[:, 0:H, :],
-            in0=bias_q[:],
-            in1=sign[:, 0:H].unsqueeze(2).to_broadcast([P, H, D]),
-            op=ALU.mult,
-        )
-        nc.vector.tensor_tensor(
-            out=bias[:, H:G, :],
-            in0=bias_k[:],
-            in1=sign[:, H:G].unsqueeze(2).to_broadcast([P, H, D]),
-            op=ALU.mult,
-        )
+        bias_rows_bf = const.tile([P, P], BF16)
+        nc.vector.memset(bias_rows_bf[:], 0.0)
+        for side, b_in in enumerate((bq, bk)):
+            for twice in range(2):
+                nc.scalar.dma_start(
+                    out=bias_rows_bf[side * H : (side + 1) * H, twice * D : (twice + 1) * D], in_=b_in
+                )
+        bias_rows = const.tile([P, P], F32)
+        nc.vector.tensor_copy(out=bias_rows[:], in_=bias_rows_bf[:])
+        bias_turned = turn_psum.tile([P, P], F32, tag="turned")
+        nc.tensor.transpose(bias_turned[:], bias_rows[:], ident_f32[:])
+        bias_col = const.tile([P, G], F32)
+        nc.vector.tensor_tensor(out=bias_col[:], in0=bias_turned[:, 0:G], in1=sign[:], op=ALU.mult)
 
         gain_rows_bf = const.tile([P, P], BF16)
         shift_rows_bf = const.tile([P, P], BF16)
@@ -183,42 +173,59 @@ def tile_multiheadselfattention_pa_kernel(
             banks = []
             for j in range(PACK):
                 conv = conv_psum.tile([P, OCT, D], F32)
+                for quarter in range(K_PASS // P):
+                    nc.tensor.matmul(
+                        out=conv[:, 2 * quarter : 2 * quarter + 2, :].rearrange("p f d -> p (f d)"),
+                        lhsT=bias_col[:, g : g + 1].to_broadcast([P, P]),
+                        rhs=ident_f32[:],
+                        is_transpose=True,
+                        start=(quarter == 0),
+                        stop=False,
+                    )
                 for f8 in range(OCT):
                     nc.tensor.matmul(
                         out=conv[:, f8, :],
                         lhsT=(x_raw[tt][:, :, j * OCT + f8] if u < FRAME_TILES else x_ft[:, j * OCT + f8, frames]),
                         rhs=w_T[:, g, :],
-                        start=True,
-                        stop=True,
+                        start=False,
+                        stop=(f8 == OCT - 1),
                     )
                 banks.append(conv)
             return banks
 
-        def add_bias(u, banks):
+        def prelu(u, banks):
             g = group_of(u)
             feat_u = feat_pool.tile([P, K], F32)
             feat[u] = feat_u
-            for j in range(PACK):
-                nc.vector.tensor_tensor(
+            parts_u = stat_pool.tile([P, PACK], F32)
+            scaled_v = []
+
+            def times_slope(j):
+                a_v = work_pool.tile([P, D, OCT], F32, bufs=3)
+                nc.vector.tensor_scalar_mul(
+                    out=a_v[:], in0=banks[j][:].rearrange("p f d -> p d f"), scalar1=slope[:, g : g + 1]
+                )
+                scaled_v.append(a_v)
+
+            def larger(j):
+                nc.vector.scalar_tensor_tensor(
                     out=feat_u[:, j * K_PASS : (j + 1) * K_PASS].rearrange("p (d f) -> p d f", f=OCT),
                     in0=banks[j][:].rearrange("p f d -> p d f"),
-                    in1=bias[:, g, :].unsqueeze(2).to_broadcast([P, D, OCT]),
-                    op=ALU.add,
+                    scalar=1.0,
+                    in1=scaled_v[j][:],
+                    op0=ALU.mult,
+                    op1=ALU.max,
+                    accum_out=parts_u[:, j : j + 1],
                 )
 
-        def prelu(u):
-            g = group_of(u)
+            times_slope(0)
+            for j in range(1, PACK):
+                times_slope(j)
+                larger(j - 1)
+            larger(PACK - 1)
             total_u = stat_pool.tile([P, 1], F32)
             total[u] = total_u
-            nc.vector.scalar_tensor_tensor(
-                out=feat[u][:],
-                in0=feat[u][:],
-                scalar=slope[:, g : g + 1],
-                in1=feat[u][:],
-                op0=ALU.mult,
-                op1=ALU.max,
-                accum_out=total_u[:],
-            )
+            nc.vector.tensor_reduce(out=total_u[:], in_=parts_u[:], axis=mybir.AxisListType.X, op=ALU.add)
 
         def squares(u):
             sq_u = stat_pool.tile([P, 1], F32)
@@ -302,35 +309,36 @@ def tile_multiheadselfattention_pa_kernel(
                     scale=gain_T[:, g, col : col + 1],
                 )
 
-        def regroup(b, split):
+        def regroup(b, first_engine, split):
             if b % 2 == 0:
                 pair = work_pool.tile([P, 2, T, PACK], BF16, align_bytes=64)
                 grouped[b // 2] = pair
             pair = grouped[b // 2]
-            nc.scalar.copy(
-                out=pair[:, b % 2, 0:split, :].rearrange("p (c i) j -> p c j i", i=4),
-                in_=planes[b][:, :, 0:split].rearrange("p j (c i) -> p c j i", i=4),
-            )
-            nc.vector.tensor_copy(
-                out=pair[:, b % 2, split:T, :].rearrange("p (c i) j -> p c j i", i=4),
-                in_=planes[b][:, :, split:T].rearrange("p j (c i) -> p c j i", i=4),
-            )
+            low_out = pair[:, b % 2, 0:split, :].rearrange("p (c i) j -> p c j i", i=4)
+            low_in = planes[b][:, :, 0:split].rearrange("p j (c i) -> p c j i", i=4)
+            high_out = pair[:, b % 2, split:T, :].rearrange("p (c i) j -> p c j i", i=4)
+            high_in = planes[b][:, :, split:T].rearrange("p j (c i) -> p c j i", i=4)
+            if first_engine == "gpsimd":
+                nc.gpsimd.tensor_scalar(
+                    out=pair[:, b % 2, 0:split, :],
+                    in0=planes[b][:, :, 0:split].rearrange("p j t -> p t j"),
+                    scalar1=1.0,
+                    scalar2=0.0,
+                    op0=ALU.mult,
+                    op1=ALU.add,
+                )
+                nc.scalar.copy(out=high_out, in_=high_in)
+            else:
+                nc.scalar.copy(out=low_out, in_=low_in)
+                nc.vector.tensor_copy(out=high_out, in_=high_in)
 
-        def quantise(pair_no):
-            i, half = pair_no // 2, pair_no % 2
-            if half == 0:
+        def quantise_pass(b):
+            i, s = b // PASSES, b % PASSES
+            if s == 0:
                 codes_i = code_pool.tile([P, PASSES, T], U32, align_bytes=64)
                 scales_i = code_pool.tile([P, PASSES, T], U8, align_bytes=64)
                 codes[i] = codes_i
                 scales[i] = scales_i
-            nc.vector.quantize_mx(
-                out=codes[i][:, 2 * half : 2 * half + 2, :].rearrange("p s t -> p (s t)").bitcast(FP8X4),
-                scales=scales[i][:, 2 * half : 2 * half + 2, :].rearrange("p s t -> p (s t)"),
-                in_=grouped[pair_no][:].rearrange("p s t j -> p (s t j)"),
-            )
-
-        def quantise_pass(b):
-            i, s = b // PASSES, b % PASSES
             nc.vector.quantize_mx(
                 out=codes[i][:, s, :].bitcast(FP8X4),
                 scales=scales[i][:, s, :],
@@ -361,37 +369,41 @@ def tile_multiheadselfattention_pa_kernel(
 
         last_acc = []
         with tc.manual_schedule():
+            conv_banks = convolve(0)
             for n in range(UNITS + LAG_TURN + 2):
                 b = n - LAG_TURN
-                vector_is_free = n > UNITS
+                vector_is_free = n >= UNITS
                 u_norm = n - 1 - LAG_STAT
                 if 0 <= u_norm < UNITS:
-                    normalise(u_norm, nc.vector if n >= UNITS else nc.gpsimd)
-                conv_banks = convolve(n) if n < UNITS else None
-                if 0 <= n - 1 < UNITS:
-                    squares(n - 1)
-                if n < UNITS:
-                    add_bias(n, conv_banks)
+                    normalise(u_norm, nc.vector if vector_is_free else nc.gpsimd)
+                if 0 <= b - 1 < UNITS and not vector_is_free:
+                    regroup(b - 1, "gpsimd", SPLIT)
                 if 0 <= b < UNITS:
                     planes_b = work_pool.tile([P, PACK, T], BF16, bufs=3)
                     planes[b] = planes_b
                     turned_banks = turn(b)
+                if n < UNITS:
+                    prelu(n, conv_banks)
+                if n + 1 < UNITS:
+                    conv_banks = convolve(n + 1)
+                if 0 <= n - 1 < UNITS:
+                    squares(n - 1)
+                if 0 <= b < UNITS:
                     gain_shift(b, 0, turned_banks[0], False)
                 if 0 <= n - 1 < UNITS:
                     inverse_deviation(n - 1)
                 if n == 0:
                     copy_x(0)
-                if n + 1 < 2 * FRAME_TILES:
-                    copy_x(n + 1)
+                    copy_x(1)
+                if n + 2 < 2 * FRAME_TILES:
+                    copy_x(n + 2)
                 if 0 <= b < UNITS:
                     gain_shift(b, 1, turned_banks[1], vector_is_free)
                     gain_shift(b, 2, turned_banks[2], False)
-                    gain_shift(b, 3, turned_banks[3], True)
-                if 0 <= b - 1 < UNITS:
-                    regroup(b - 1, SPLIT_END if vector_is_free else SPLIT)
-                if b % 2 == 1 and 0 <= b - 3 < UNITS - 2:
-                    quantise((b - 3) // 2)
-                if UNITS <= b:
+                    gain_shift(b, 3, turned_banks[3], vector_is_free)
+                if 0 <= b - 1 < UNITS and vector_is_free:
+                    regroup(b - 1, "scalar", SPLIT_END)
+                if 0 <= b - 2 < UNITS:
                     quantise_pass(b - 2)
                 if n == 2:
                     turn_tables()
@@ -399,8 +411,6 @@ def tile_multiheadselfattention_pa_kernel(
                     finish_tables()
                 if 0 <= n - LAG_STAT < UNITS:
                     release(n - LAG_STAT)
-                if n < UNITS:
-                    prelu(n)
                 r = b - 6
                 if 0 <= r < UNITS - FRAME_TILES and (r // FRAME_TILES) % 2 == 1:
                     if n < UNITS:
@@ -409,14 +419,12 @@ def tile_multiheadselfattention_pa_kernel(
                         acc = conv_psum.tile([P, T], F32, tag="conv")
                     score_passes(r // (2 * FRAME_TILES), r % FRAME_TILES, acc, range(PASSES))
                     store_scores(r // (2 * FRAME_TILES), r % FRAME_TILES, acc, vector_is_free and r % 2 == 1)
-                if b == UNITS - 1:
+                if UNITS - PASSES <= b - 2 < UNITS:
                     for tt in range(FRAME_TILES):
-                        acc = conv_psum.tile([P, T], F32, tag="conv")
-                        last_acc.append(acc)
-                        score_passes(H - 1, tt, acc, (0, 1))
-                if UNITS <= b:
-                    for tt in range(FRAME_TILES):
-                        score_passes(H - 1, tt, last_acc[tt], (b - UNITS + 2,))
-                if b == UNITS + 1:
+                        if b - 2 == UNITS - PASSES:
+                            acc = conv_psum.tile([P, T], F32, tag="conv")
+                            last_acc.append(acc)
+                        score_passes(H - 1, tt, last_acc[tt], ((b - 2) % PASSES,))
+                if b - 2 == UNITS - 1:
                     for tt in range(FRAME_TILES):
                         store_scores(H - 1, tt, last_acc[tt], tt % 2 == 1)

@@ -147,6 +147,7 @@ def tile_multiheadselfattention_pa_kernel(
             )
 
         feat = {}
+        parts = {}
         total = {}
         sq_total = {}
         rstd = {}
@@ -198,6 +199,7 @@ def tile_multiheadselfattention_pa_kernel(
             feat_u = feat_pool.tile([P, K], F32)
             feat[u] = feat_u
             parts_u = stat_pool.tile([P, PACK], F32)
+            parts[u] = parts_u
             scaled_v = []
 
             def times_slope(j):
@@ -223,9 +225,11 @@ def tile_multiheadselfattention_pa_kernel(
                 times_slope(j)
                 larger(j - 1)
             larger(PACK - 1)
+
+        def sum_parts(u):
             total_u = stat_pool.tile([P, 1], F32)
             total[u] = total_u
-            nc.vector.tensor_reduce(out=total_u[:], in_=parts_u[:], axis=mybir.AxisListType.X, op=ALU.add)
+            nc.vector.tensor_reduce(out=total_u[:], in_=parts[u][:], axis=mybir.AxisListType.X, op=ALU.add)
 
         def squares(u):
             sq_u = stat_pool.tile([P, 1], F32)
@@ -374,10 +378,17 @@ def tile_multiheadselfattention_pa_kernel(
                 b = n - LAG_TURN
                 vector_is_free = n >= UNITS
                 u_norm = n - 1 - LAG_STAT
+                r = b - 6
+                scores_due = 0 <= r < UNITS - FRAME_TILES and (r // FRAME_TILES) % 2 == 1
                 if 0 <= u_norm < UNITS:
                     normalise(u_norm, nc.vector if vector_is_free else nc.gpsimd)
+                if 0 <= n - 1 < UNITS:
+                    squares(n - 1)
                 if 0 <= b - 1 < UNITS and not vector_is_free:
                     regroup(b - 1, "gpsimd", SPLIT)
+                if scores_due and not vector_is_free:
+                    acc = turn_psum.tile([P, T], F32, tag="turned")
+                    score_passes(r // (2 * FRAME_TILES), r % FRAME_TILES, acc, range(PASSES))
                 if 0 <= b < UNITS:
                     planes_b = work_pool.tile([P, PACK, T], BF16, bufs=3)
                     planes[b] = planes_b
@@ -386,8 +397,8 @@ def tile_multiheadselfattention_pa_kernel(
                     prelu(n, conv_banks)
                 if n + 1 < UNITS:
                     conv_banks = convolve(n + 1)
-                if 0 <= n - 1 < UNITS:
-                    squares(n - 1)
+                if scores_due and not vector_is_free:
+                    store_scores(r // (2 * FRAME_TILES), r % FRAME_TILES, acc, False)
                 if 0 <= b < UNITS:
                     gain_shift(b, 0, turned_banks[0], False)
                 if 0 <= n - 1 < UNITS:
@@ -405,20 +416,18 @@ def tile_multiheadselfattention_pa_kernel(
                     regroup(b - 1, "scalar", SPLIT_END)
                 if 0 <= b - 2 < UNITS:
                     quantise_pass(b - 2)
+                if n < UNITS:
+                    sum_parts(n)
                 if n == 2:
                     turn_tables()
                 if n == 4:
                     finish_tables()
                 if 0 <= n - LAG_STAT < UNITS:
                     release(n - LAG_STAT)
-                r = b - 6
-                if 0 <= r < UNITS - FRAME_TILES and (r // FRAME_TILES) % 2 == 1:
-                    if n < UNITS:
-                        acc = turn_psum.tile([P, T], F32, tag="turned")
-                    else:
-                        acc = conv_psum.tile([P, T], F32, tag="conv")
+                if scores_due and vector_is_free:
+                    acc = conv_psum.tile([P, T], F32, tag="conv")
                     score_passes(r // (2 * FRAME_TILES), r % FRAME_TILES, acc, range(PASSES))
-                    store_scores(r // (2 * FRAME_TILES), r % FRAME_TILES, acc, vector_is_free and r % 2 == 1)
+                    store_scores(r // (2 * FRAME_TILES), r % FRAME_TILES, acc, r % 2 == 1)
                 if UNITS - PASSES <= b - 2 < UNITS:
                     for tt in range(FRAME_TILES):
                         if b - 2 == UNITS - PASSES:

@@ -386,6 +386,8 @@ def tile_multiheadselfattention_pa_kernel(
                     squares(n - 1)
                 if 0 <= b - 1 < UNITS and not vector_is_free:
                     regroup(b - 1, "gpsimd", SPLIT)
+                if 0 <= n - 1 < UNITS:
+                    inverse_deviation(n - 1)
                 if scores_due and not vector_is_free:
                     acc = turn_psum.tile([P, T], F32, tag="turned")
                     score_passes(r // (2 * FRAME_TILES), r % FRAME_TILES, acc, range(PASSES))
@@ -401,8 +403,6 @@ def tile_multiheadselfattention_pa_kernel(
                     store_scores(r // (2 * FRAME_TILES), r % FRAME_TILES, acc, False)
                 if 0 <= b < UNITS:
                     gain_shift(b, 0, turned_banks[0], False)
-                if 0 <= n - 1 < UNITS:
-                    inverse_deviation(n - 1)
                 if n == 0:
                     copy_x(0)
                     copy_x(1)
@@ -414,16 +414,16 @@ def tile_multiheadselfattention_pa_kernel(
                     gain_shift(b, 3, turned_banks[3], vector_is_free)
                 if 0 <= b - 1 < UNITS and vector_is_free:
                     regroup(b - 1, "scalar", SPLIT_END)
-                if 0 <= b - 2 < UNITS:
-                    quantise_pass(b - 2)
-                if n < UNITS:
-                    sum_parts(n)
                 if n == 2:
                     turn_tables()
                 if n == 4:
                     finish_tables()
                 if 0 <= n - LAG_STAT < UNITS:
                     release(n - LAG_STAT)
+                if 0 <= b - 2 < UNITS:
+                    quantise_pass(b - 2)
+                if n < UNITS:
+                    sum_parts(n)
                 if scores_due and vector_is_free:
                     acc = conv_psum.tile([P, T], F32, tag="conv")
                     score_passes(r // (2 * FRAME_TILES), r % FRAME_TILES, acc, range(PASSES))

@@ -50,6 +50,10 @@ def tile_multiheadselfattention_pa_kernel(
         conv_psum = ctx.enter_context(tc.psum_pool(name="convp", bufs=4))
         turn_psum = ctx.enter_context(tc.psum_pool(name="turnp", bufs=4))
 
+        bias_rows_bf = const.tile([P, D], BF16)
+        nc.vector.memset(bias_rows_bf[:], 0.0)
+        nc.sync.dma_start(out=bias_rows_bf[0:H, :], in_=bq)
+        nc.sync.dma_start(out=bias_rows_bf[H:G, :], in_=bk)
         ident_f32 = const.tile([P, P], F32)
         make_identity(nc, ident_f32[:])
         ident_bf = const.tile([P, P], BF16)
@@ -95,15 +99,9 @@ def tile_multiheadselfattention_pa_kernel(
             nc.sync.dma_start(out=raw[:], in_=x[0, :, tt * P : (tt + 1) * P, :])
             x_raw.append(raw)
 
-        bias_rows_bf = const.tile([P, P], BF16)
-        nc.vector.memset(bias_rows_bf[:], 0.0)
-        for side, b_in in enumerate((bq, bk)):
-            for twice in range(2):
-                nc.scalar.dma_start(
-                    out=bias_rows_bf[side * H : (side + 1) * H, twice * D : (twice + 1) * D], in_=b_in
-                )
         bias_rows = const.tile([P, P], F32)
-        nc.vector.tensor_copy(out=bias_rows[:], in_=bias_rows_bf[:])
+        for twice in range(2):
+            nc.vector.tensor_copy(out=bias_rows[:, twice * D : (twice + 1) * D], in_=bias_rows_bf[:])
         bias_turned = turn_psum.tile([P, P], F32, tag="turned")
         nc.tensor.transpose(bias_turned[:], bias_rows[:], ident_f32[:])
         bias_col = const.tile([P, G], F32)

@@ -31,7 +31,7 @@ LAG_TURN = 6
 LAG_STAT = 1
 FEAT_BUFS = 12
 SPLIT = 416
-SPLIT_END = 256
+SPLIT_END = 320
 
 FLOPS = 2 * C * (G * D) * (T * F) + 2 * H * T * T * K
 
@@ -382,8 +382,8 @@ def tile_multiheadselfattention_pa_kernel(
                     normalise(u_norm, nc.vector if vector_is_free else nc.gpsimd)
                 if 0 <= n - 1 < UNITS:
                     squares(n - 1)
-                if 0 <= b - 1 < UNITS and not vector_is_free:
-                    regroup(b - 1, "gpsimd", SPLIT)
+                if 0 <= b - 1 < UNITS - 1:
+                    regroup(b - 1, "gpsimd", SPLIT_END if vector_is_free else SPLIT)
                 if 0 <= n - 1 < UNITS:
                     inverse_deviation(n - 1)
                 if scores_due and not vector_is_free:
@@ -410,8 +410,8 @@ def tile_multiheadselfattention_pa_kernel(
                     gain_shift(b, 1, turned_banks[1], vector_is_free)
                     gain_shift(b, 2, turned_banks[2], False)
                     gain_shift(b, 3, turned_banks[3], vector_is_free)
-                if 0 <= b - 1 < UNITS and vector_is_free:
-                    regroup(b - 1, "scalar", SPLIT_END)
+                if b - 1 == UNITS - 1:
+                    regroup(b - 1, "scalar", T // 2)
                 if n == 2:
                     turn_tables()
                 if n == 4:

@@ -159,11 +159,20 @@ def tile_multiheadselfattention_pa_kernel(
             i = u // FRAME_TILES
             return (i % 2) * H + i // 2
 
-        def copy_x(half):
-            tt, first = half // 2, (half % 2) * (F // 2)
+        def copy_x_scalar(tt, first, count):
             nc.scalar.copy(
-                out=x_ft[:, first : first + F // 2, tt * P : (tt + 1) * P].rearrange("c (q i) t -> c q t i", i=4),
-                in_=x_raw[tt][:, :, first : first + F // 2].rearrange("c t (q i) -> c q t i", i=4),
+                out=x_ft[:, first : first + count, tt * P : (tt + 1) * P].rearrange("c (q i) t -> c q t i", i=4),
+                in_=x_raw[tt][:, :, first : first + count].rearrange("c t (q i) -> c q t i", i=4),
+            )
+
+        def copy_x_gpsimd(tt, first, count):
+            nc.gpsimd.tensor_scalar(
+                out=x_ft[:, first : first + count, tt * P : (tt + 1) * P],
+                in0=x_raw[tt][:, :, first : first + count].rearrange("c t f -> c f t"),
+                scalar1=1.0,
+                scalar2=0.0,
+                op0=ALU.mult,
+                op1=ALU.add,
             )
 
         def convolve(u):
@@ -171,7 +180,10 @@ def tile_multiheadselfattention_pa_kernel(
             frames = slice(tt * P, (tt + 1) * P)
             banks = []
             for j in range(PACK):
-                conv = conv_psum.tile([P, OCT, D], F32)
+                if u < LAG_TURN and u % 2 == 1:
+                    conv = turn_psum.tile([P, OCT, D], F32, tag="turned")
+                else:
+                    conv = conv_psum.tile([P, OCT, D], F32, tag="conv")
                 for quarter in range(K_PASS // P):
                     nc.tensor.matmul(
                         out=conv[:, 2 * quarter : 2 * quarter + 2, :].rearrange("p f d -> p (f d)"),
@@ -192,20 +204,22 @@ def tile_multiheadselfattention_pa_kernel(
                 banks.append(conv)
             return banks
 
-        def prelu(u, banks):
+        def prelu(u, banks, scalar_banks, between):
             g = group_of(u)
             feat_u = feat_pool.tile([P, K], F32)
             feat[u] = feat_u
             parts_u = stat_pool.tile([P, PACK], F32)
             parts[u] = parts_u
-            scaled_v = []
+            scaled_v = [None] * PACK
 
             def times_slope(j):
-                a_v = work_pool.tile([P, D, OCT], F32, bufs=3)
-                nc.vector.tensor_scalar_mul(
-                    out=a_v[:], in0=banks[j][:].rearrange("p f d -> p d f"), scalar1=slope[:, g : g + 1]
-                )
-                scaled_v.append(a_v)
+                a_v = work_pool.tile([P, D, OCT], F32, bufs=4)
+                v = banks[j][:].rearrange("p f d -> p d f")
+                if j < PACK - scalar_banks:
+                    nc.vector.tensor_scalar_mul(out=a_v[:], in0=v, scalar1=slope[:, g : g + 1])
+                else:
+                    nc.scalar.activation(out=a_v[:], in_=v, func=ACT.Copy, scale=slope[:, g : g + 1])
+                scaled_v[j] = a_v
 
             def larger(j):
                 nc.vector.scalar_tensor_tensor(
@@ -218,9 +232,14 @@ def tile_multiheadselfattention_pa_kernel(
                     accum_out=parts_u[:, j : j + 1],
                 )
 
+            for j in range(PACK - scalar_banks, PACK):
+                times_slope(j)
+            if between is not None:
+                between()
             times_slope(0)
             for j in range(1, PACK):
-                times_slope(j)
+                if j < PACK - scalar_banks:
+                    times_slope(j)
                 larger(j - 1)
             larger(PACK - 1)
 
@@ -378,13 +397,17 @@ def tile_multiheadselfattention_pa_kernel(
                 u_norm = n - 1 - LAG_STAT
                 r = b - 6
                 scores_due = 0 <= r < UNITS - FRAME_TILES and (r // FRAME_TILES) % 2 == 1
-                if 0 <= u_norm < UNITS:
+                if n == 3:
+                    normalise(0, nc.gpsimd)
+                if 0 <= u_norm < UNITS and n >= 3:
                     normalise(u_norm, nc.vector if vector_is_free else nc.gpsimd)
-                if 0 <= n - 1 < UNITS:
+                early = n < LAG_TURN
+                copies_x = 1 <= n <= FRAME_TILES
+                if 0 <= n - 1 < UNITS and not early:
                     squares(n - 1)
                 if 0 <= b - 1 < UNITS - 1:
                     regroup(b - 1, "gpsimd", SPLIT_END if vector_is_free else SPLIT)
-                if 0 <= n - 1 < UNITS:
+                if 0 <= n - 1 < UNITS and not early:
                     inverse_deviation(n - 1)
                 if scores_due and not vector_is_free:
                     acc = turn_psum.tile([P, T], F32, tag="turned")
@@ -394,25 +417,28 @@ def tile_multiheadselfattention_pa_kernel(
                     planes[b] = planes_b
                     turned_banks = turn(b)
                 if n < UNITS:
-                    prelu(n, conv_banks)
+                    def stats():
+                        if n > 0:
+                            squares(n - 1)
+                            inverse_deviation(n - 1)
+                    prelu(n, conv_banks, (1 if copies_x else 2) if early else 0, stats if early else None)
                 if n + 1 < UNITS:
                     conv_banks = convolve(n + 1)
                 if scores_due and not vector_is_free:
                     store_scores(r // (2 * FRAME_TILES), r % FRAME_TILES, acc, False)
                 if 0 <= b < UNITS:
                     gain_shift(b, 0, turned_banks[0], False)
-                if n == 0:
-                    copy_x(0)
-                    copy_x(1)
-                if n + 2 < 2 * FRAME_TILES:
-                    copy_x(n + 2)
+                if n < FRAME_TILES - 1:
+                    copy_x_gpsimd(n, 0, F)
+                if copies_x:
+                    copy_x_scalar(FRAME_TILES - 1, (n - 1) * (F // 4), F // 4)
                 if 0 <= b < UNITS:
                     gain_shift(b, 1, turned_banks[1], vector_is_free)
                     gain_shift(b, 2, turned_banks[2], False)
                     gain_shift(b, 3, turned_banks[3], vector_is_free)
                 if b - 1 == UNITS - 1:
                     regroup(b - 1, "scalar", T // 2)
-                if n == 2:
+                if n == 3:
                     turn_tables()
                 if n == 4:
                     finish_tables()

@@ -68,6 +68,11 @@ def tile_multiheadselfattention_pa_kernel(
         nc.scalar.dma_start(out=slope_q[:], in_=aq.partition_broadcast(P))
         slope_k = const.tile([P, H], BF16)
         nc.scalar.dma_start(out=slope_k[:], in_=ak.partition_broadcast(P))
+        table_col = const.tile([P, 1], F32)
+        nc.scalar.activation(
+            out=table_col[:], in_=zero_col[:], func=ACT.Abs_reciprocal_sqrt, bias=eps_col[:], scale=1.0
+        )
+
         slope = const.tile([P, G], F32)
         nc.vector.tensor_copy(out=slope[:, 0:H], in_=slope_q[:])
         nc.vector.tensor_copy(out=slope[:, H:G], in_=slope_k[:])
@@ -77,6 +82,9 @@ def tile_multiheadselfattention_pa_kernel(
             out=sign[:], in0=slope[:], scalar1=1.0, scalar2=-2.0, op0=ALU.is_gt, op1=ALU.mult
         )
         nc.vector.tensor_scalar_add(out=sign[:], in0=sign[:], scalar1=1.0)
+
+        first_sign = const.tile([P, 1], BF16)
+        nc.vector.tensor_tensor(out=first_sign[:], in0=ident_bf[:, 0:1], in1=sign[:, 0:1], op=ALU.mult)
 
         w_rows = const.tile([P, 4, C], BF16)
         nc.sync.dma_start(out=w_rows[:, 0:2, :], in_=Wq.rearrange("(a h) d c -> (h d) a c", a=2))
@@ -125,10 +133,14 @@ def tile_multiheadselfattention_pa_kernel(
         shift_T = const.tile([P, G, PASSES * PACK], F32)
         tables = []
 
+        def cast_tables():
+            for rows, rows_bf in ((gain_rows, gain_rows_bf), (shift_rows, shift_rows_bf)):
+                nc.gpsimd.tensor_scalar(
+                    out=rows[:], in0=rows_bf[:], scalar1=1.0, scalar2=0.0, op0=ALU.mult, op1=ALU.add
+                )
+
         def turn_tables():
-            nc.vector.tensor_copy(out=gain_rows[:], in_=gain_rows_bf[:])
-            nc.vector.tensor_copy(out=shift_rows[:], in_=shift_rows_bf[:])
-            table_turned = turn_psum.tile([P, 2, P], F32, tag="turned")
+            table_turned = conv_psum.tile([P, 2, P], F32, tag="conv")
             nc.tensor.transpose(table_turned[:, 0, :], gain_rows[:], ident_f32[:])
             nc.tensor.transpose(table_turned[:, 1, :], shift_rows[:], ident_f32[:])
             tables.append(table_turned)
@@ -176,23 +188,44 @@ def tile_multiheadselfattention_pa_kernel(
             )
 
         def convolve(u):
-            g, tt = group_of(u), u % FRAME_TILES
-            frames = slice(tt * P, (tt + 1) * P)
+            g = group_of(u)
             banks = []
             for j in range(PACK):
                 if u < LAG_TURN and u % 2 == 1:
                     conv = turn_psum.tile([P, OCT, D], F32, tag="turned")
                 else:
                     conv = conv_psum.tile([P, OCT, D], F32, tag="conv")
-                for quarter in range(K_PASS // P):
+                banks.append(conv)
+                if u == 0 and j >= 2:
+                    convolve_bank(u, j - 2, banks[j - 2])
+                if u < FRAME_TILES:
                     nc.tensor.matmul(
-                        out=conv[:, 2 * quarter : 2 * quarter + 2, :].rearrange("p f d -> p (f d)"),
-                        lhsT=bias_col[:, g : g + 1].to_broadcast([P, P]),
-                        rhs=ident_f32[:],
-                        is_transpose=True,
-                        start=(quarter == 0),
+                        out=conv[:],
+                        lhsT=first_sign[:].to_broadcast([P, P]),
+                        rhs=bias_rows_bf[:].unsqueeze(1).to_broadcast([P, OCT, D]),
+                        start=True,
                         stop=False,
                     )
+                else:
+                    for quarter in range(K_PASS // P):
+                        nc.tensor.matmul(
+                            out=conv[:, 2 * quarter : 2 * quarter + 2, :].rearrange("p f d -> p (f d)"),
+                            lhsT=bias_col[:, g : g + 1].to_broadcast([P, P]),
+                            rhs=ident_f32[:],
+                            is_transpose=True,
+                            start=(quarter == 0),
+                            stop=False,
+                        )
+                if u > 0:
+                    convolve_bank(u, j, conv)
+            if u == 0:
+                convolve_bank(u, 2, banks[2])
+                convolve_bank(u, 3, banks[3])
+            return banks
+
+        def convolve_bank(u, j, conv):
+                g, tt = group_of(u), u % FRAME_TILES
+                frames = slice(tt * P, (tt + 1) * P)
                 for f8 in range(OCT):
                     nc.tensor.matmul(
                         out=conv[:, f8, :],
@@ -201,8 +234,6 @@ def tile_multiheadselfattention_pa_kernel(
                         start=False,
                         stop=(f8 == OCT - 1),
                     )
-                banks.append(conv)
-            return banks
 
         def prelu(u, banks, scalar_banks, between):
             g = group_of(u)
@@ -275,14 +306,26 @@ def tile_multiheadselfattention_pa_kernel(
         def release(u):
             offset_u = stat_pool.tile([P, 1], F32)
             offset[u] = offset_u
-            nc.vector.tensor_scalar(
-                out=offset_u[:],
-                in0=total[u][:],
-                scalar1=rstd[u][:],
-                scalar2=-1.0 / K,
-                op0=ALU.mult,
-                op1=ALU.mult,
-            )
+            if u < LAG_TURN:
+                product_u = stat_pool.tile([P, 1], F32)
+                nc.vector.tensor_scalar(
+                    out=product_u[:],
+                    in0=total[u][:],
+                    scalar1=rstd[u][:],
+                    scalar2=-1.0 / K,
+                    op0=ALU.mult,
+                    op1=ALU.mult,
+                    accum_out=offset_u[:],
+                )
+            else:
+                nc.vector.tensor_scalar(
+                    out=offset_u[:],
+                    in0=total[u][:],
+                    scalar1=rstd[u][:],
+                    scalar2=-1.0 / K,
+                    op0=ALU.mult,
+                    op1=ALU.mult,
+                )
 
         def normalise(u, engine):
             engine.tensor_scalar(
@@ -416,6 +459,8 @@ def tile_multiheadselfattention_pa_kernel(
                     planes_b = work_pool.tile([P, PACK, T], BF16, bufs=3)
                     planes[b] = planes_b
                     turned_banks = turn(b)
+                if n == 3:
+                    finish_tables()
                 if n < UNITS:
                     def stats():
                         if n > 0:
@@ -438,10 +483,10 @@ def tile_multiheadselfattention_pa_kernel(
                     gain_shift(b, 3, turned_banks[3], vector_is_free)
                 if b - 1 == UNITS - 1:
                     regroup(b - 1, "scalar", T // 2)
-                if n == 3:
+                if n == 1:
+                    cast_tables()
+                if n == 2:
                     turn_tables()
-                if n == 4:
-                    finish_tables()
                 if 0 <= n - LAG_STAT < UNITS:
                     release(n - LAG_STAT)
                 if 0 <= b - 2 < UNITS:

@@ -100,7 +100,7 @@ def tile_multiheadselfattention_pa_kernel(
             op=ALU.mult,
         )
 
-        x_ft = const.tile([P, F, T], BF16)
+        x_ft = const.tile([P, F // 2, T, 2], BF16)
         x_raw = []
         for tt in range(FRAME_TILES):
             raw = feat_pool.tile([P, P, F], BF16, tag="feat_u")
@@ -171,20 +171,13 @@ def tile_multiheadselfattention_pa_kernel(
             i = u // FRAME_TILES
             return (i % 2) * H + i // 2
 
-        def copy_x_scalar(tt, first, count):
+        def copy_x(tt, first, count):
             nc.scalar.copy(
-                out=x_ft[:, first : first + count, tt * P : (tt + 1) * P].rearrange("c (q i) t -> c q t i", i=4),
-                in_=x_raw[tt][:, :, first : first + count].rearrange("c t (q i) -> c q t i", i=4),
-            )
-
-        def copy_x_gpsimd(tt, first, count):
-            nc.gpsimd.tensor_scalar(
-                out=x_ft[:, first : first + count, tt * P : (tt + 1) * P],
-                in0=x_raw[tt][:, :, first : first + count].rearrange("c t f -> c f t"),
-                scalar1=1.0,
-                scalar2=0.0,
-                op0=ALU.mult,
-                op1=ALU.add,
+                out=x_ft[:, first : first + count, tt * P : (tt + 1) * P, :]
+                .rearrange("c f t e -> c f (t e)")
+                .bitcast(F32)
+                .rearrange("c (q i) t -> c q t i", i=4),
+                in_=x_raw[tt][:].bitcast(F32)[:, :, first : first + count].rearrange("c t (q i) -> c q t i", i=4),
             )
 
         def convolve(u):
@@ -229,7 +222,7 @@ def tile_multiheadselfattention_pa_kernel(
                 for f8 in range(OCT):
                     nc.tensor.matmul(
                         out=conv[:, f8, :],
-                        lhsT=(x_raw[tt][:, :, j * OCT + f8] if u < FRAME_TILES else x_ft[:, j * OCT + f8, frames]),
+                        lhsT=(x_raw[tt][:, :, j * OCT + f8] if u < FRAME_TILES else x_ft[:, (j * OCT + f8) // 2, frames, f8 % 2]),
                         rhs=w_T[:, g, :],
                         start=False,
                         stop=(f8 == OCT - 1),
@@ -306,26 +299,14 @@ def tile_multiheadselfattention_pa_kernel(
         def release(u):
             offset_u = stat_pool.tile([P, 1], F32)
             offset[u] = offset_u
-            if u < LAG_TURN:
-                product_u = stat_pool.tile([P, 1], F32)
-                nc.vector.tensor_scalar(
-                    out=product_u[:],
-                    in0=total[u][:],
-                    scalar1=rstd[u][:],
-                    scalar2=-1.0 / K,
-                    op0=ALU.mult,
-                    op1=ALU.mult,
-                    accum_out=offset_u[:],
-                )
-            else:
-                nc.vector.tensor_scalar(
-                    out=offset_u[:],
-                    in0=total[u][:],
-                    scalar1=rstd[u][:],
-                    scalar2=-1.0 / K,
-                    op0=ALU.mult,
-                    op1=ALU.mult,
-                )
+            nc.vector.tensor_scalar(
+                out=offset_u[:],
+                in0=total[u][:],
+                scalar1=rstd[u][:],
+                scalar2=-1.0 / K,
+                op0=ALU.mult,
+                op1=ALU.mult,
+            )
 
         def normalise(u, engine):
             engine.tensor_scalar(
@@ -440,12 +421,9 @@ def tile_multiheadselfattention_pa_kernel(
                 u_norm = n - 1 - LAG_STAT
                 r = b - 6
                 scores_due = 0 <= r < UNITS - FRAME_TILES and (r // FRAME_TILES) % 2 == 1
-                if n == 3:
-                    normalise(0, nc.gpsimd)
-                if 0 <= u_norm < UNITS and n >= 3:
+                if 0 <= u_norm < UNITS:
                     normalise(u_norm, nc.vector if vector_is_free else nc.gpsimd)
                 early = n < LAG_TURN
-                copies_x = 1 <= n <= FRAME_TILES
                 if 0 <= n - 1 < UNITS and not early:
                     squares(n - 1)
                 if 0 <= b - 1 < UNITS - 1:
@@ -466,17 +444,18 @@ def tile_multiheadselfattention_pa_kernel(
                         if n > 0:
                             squares(n - 1)
                             inverse_deviation(n - 1)
-                    prelu(n, conv_banks, (1 if copies_x else 2) if early else 0, stats if early else None)
+                    prelu(n, conv_banks, 1 if early else 0, stats if early else None)
                 if n + 1 < UNITS:
                     conv_banks = convolve(n + 1)
                 if scores_due and not vector_is_free:
                     store_scores(r // (2 * FRAME_TILES), r % FRAME_TILES, acc, False)
                 if 0 <= b < UNITS:
                     gain_shift(b, 0, turned_banks[0], False)
-                if n < FRAME_TILES - 1:
-                    copy_x_gpsimd(n, 0, F)
-                if copies_x:
-                    copy_x_scalar(FRAME_TILES - 1, (n - 1) * (F // 4), F // 4)
+                if n == 0:
+                    copy_x(0, 0, F // 2)
+                    copy_x(1, 0, F // 4)
+                elif n + 2 < 2 * FRAME_TILES:
+                    copy_x((n + 2) // 2, (n + 2) % 2 * (F // 4), F // 4)
                 if 0 <= b < UNITS:
                     gain_shift(b, 1, turned_banks[1], vector_is_free)
                     gain_shift(b, 2, turned_banks[2], False)

@@ -27,7 +27,7 @@ K_PASS = P * PACK
 PASSES = K // K_PASS
 OCT = F // PACK
 UNITS = G * FRAME_TILES
-LAG_TURN = 6
+LAG_TURN = 5
 LAG_STAT = 1
 FEAT_BUFS = 12
 SPLIT = 416
@@ -45,7 +45,7 @@ def tile_multiheadselfattention_pa_kernel(
         feat_pool = ctx.enter_context(tc.tile_pool(name="feat", bufs=FEAT_BUFS))
         stat_pool = ctx.enter_context(tc.tile_pool(name="stat", bufs=8))
         work_pool = ctx.enter_context(tc.tile_pool(name="work", bufs=2))
-        code_pool = ctx.enter_context(tc.tile_pool(name="code", bufs=3))
+        code_pool = ctx.enter_context(tc.tile_pool(name="code", bufs=4))
         out_pool = ctx.enter_context(tc.tile_pool(name="outp", bufs=FRAME_TILES))
         conv_psum = ctx.enter_context(tc.psum_pool(name="convp", bufs=4))
         turn_psum = ctx.enter_context(tc.psum_pool(name="turnp", bufs=4))
@@ -228,7 +228,7 @@ def tile_multiheadselfattention_pa_kernel(
                         stop=(f8 == OCT - 1),
                     )
 
-        def prelu(u, banks, scalar_banks, between):
+        def prelu(u, banks, scalar_banks, between, before_last=None):
             g = group_of(u)
             feat_u = feat_pool.tile([P, K], F32)
             feat[u] = feat_u
@@ -265,6 +265,8 @@ def tile_multiheadselfattention_pa_kernel(
                 if j < PACK - scalar_banks:
                     times_slope(j)
                 larger(j - 1)
+                if j == 2 and before_last is not None:
+                    before_last()
             larger(PACK - 1)
 
         def sum_parts(u):
@@ -390,98 +392,255 @@ def tile_multiheadselfattention_pa_kernel(
                 in_=grouped[b // 2][:, b % 2, :, :].rearrange("p t j -> p (t j)"),
             )
 
-        def score_passes(h, tt, acc, passes):
+        def score_passes(h, tt, acc, passes, keys=slice(0, T)):
             frames = slice(tt * P, (tt + 1) * P)
             for s in passes:
                 nc.tensor.matmul_mx(
                     out=acc[:],
                     lhsT=codes[2 * h][:, s, frames].bitcast(FP8X4),
                     lhsT_scale=scales[2 * h][:, s, frames],
-                    rhs=codes[2 * h + 1][:, s, :].bitcast(FP8X4),
-                    rhs_scale=scales[2 * h + 1][:, s, :],
+                    rhs=codes[2 * h + 1][:, s, keys].bitcast(FP8X4),
+                    rhs_scale=scales[2 * h + 1][:, s, keys],
                     start=(s == 0),
                     stop=(s == PASSES - 1),
                 )
 
-        def store_scores(h, tt, acc, on_vector):
+        def store_scores(h, tt, acc, on_vector, keys=slice(0, T)):
             frames = slice(tt * P, (tt + 1) * P)
-            scaled = out_pool.tile([P, T], F32)
+            scaled = out_pool.tile([P, keys.stop - keys.start], F32)
             if on_vector:
                 nc.vector.tensor_scalar_mul(out=scaled[:], in0=acc[:], scalar1=1.0 / math.sqrt(K))
             else:
                 nc.scalar.mul(out=scaled[:], in_=acc[:], mul=1.0 / math.sqrt(K))
-            nc.sync.dma_start(out=out[0, h, frames, :], in_=scaled[:])
+            nc.sync.dma_start(out=out[0, h, frames, keys], in_=scaled[:])
 
-        last_acc = []
+        k3 = (G - 1) * PASSES
+        late = {}
+        late_codes = {}
+        halves = list(range(1, 8))
+
+        def head2_scores(count):
+            accs = []
+            for x in halves[:count]:
+                tt, keys = x // 2, slice(x % 2 * (T // 2), x % 2 * (T // 2) + (T // 2))
+                acc = conv_psum.tile([P, (T // 2)], F32, tag="conv")
+                score_passes(2, tt, acc, range(PASSES), keys)
+                accs.append((tt, acc, keys))
+            for i in range(len(accs)):
+                halves.remove(halves[0])
+            return accs
+
+        def late_turn(u):
+            planes_u = work_pool.tile([P, PASSES, PACK, P], BF16, tag="planes_b", bufs=3)
+            banks = []
+            for s in range(PASSES):
+                turned = turn_psum.tile([P, PACK, P], F32, tag="turned")
+                for j in range(PACK):
+                    first = j * K_PASS + s * P
+                    nc.tensor.transpose(turned[:, j, :], feat[u][:, first : first + P], ident_f32[:])
+                banks.append(turned)
+            late[u] = (planes_u, banks)
+
+        def late_gain(u, s, j, on_vector):
+            planes_u, banks = late[u]
+            g, col = group_of(u), s * PACK + j
+            if on_vector:
+                nc.vector.tensor_scalar(
+                    out=planes_u[:, s, j, :], in0=banks[s][:, j, :],
+                    scalar1=gain_T[:, g, col : col + 1], scalar2=shift_T[:, g, col : col + 1],
+                    op0=ALU.mult, op1=ALU.add,
+                )
+            else:
+                nc.scalar.activation(
+                    out=planes_u[:, s, j, :], in_=banks[s][:, j, :], func=ACT.Identity,
+                    bias=shift_T[:, g, col : col + 1], scale=gain_T[:, g, col : col + 1],
+                )
+
+        def late_regroup(u):
+            grouped_u = work_pool.tile([P, PASSES, P, PACK], BF16, tag="pair", align_bytes=64)
+            grouped[u] = grouped_u
+            for s in range(PASSES):
+                o = grouped_u[:, s, :, :].rearrange("p (c i) j -> p c j i", i=4)
+                i = late[u][0][:, s, :, :].rearrange("p j (c i) -> p c j i", i=4)
+                if s < 2:
+                    nc.scalar.copy(out=o, in_=i)
+                else:
+                    nc.vector.tensor_copy(out=o, in_=i)
+
+        def late_quantise(u):
+            codes_u = code_pool.tile([P, PASSES, P], U32, tag="codes_u", bufs=2, align_bytes=64)
+            scales_u = code_pool.tile([P, PASSES, P], U8, tag="scales_u", bufs=2, align_bytes=64)
+            nc.vector.quantize_mx(
+                out=codes_u[:].rearrange("p s t -> p (s t)").bitcast(FP8X4),
+                scales=scales_u[:].rearrange("p s t -> p (s t)"),
+                in_=grouped[u][:].rearrange("p s t j -> p (s t j)"),
+            )
+            late_codes[u] = (codes_u, scales_u)
+
+        def late_scores(u):
+            codes_u, scales_u = late_codes[u]
+            accs = []
+            for tt in range(FRAME_TILES):
+                if tt % 2 == 0:
+                    acc = conv_psum.tile([P, 2, P], F32, tag="conv")
+                    accs.append(acc)
+                frames = slice(tt * P, (tt + 1) * P)
+                for s in range(PASSES):
+                    nc.tensor.matmul_mx(
+                        out=acc[:, tt % 2, :],
+                        lhsT=codes[2 * H - 2][:, s, frames].bitcast(FP8X4),
+                        lhsT_scale=scales[2 * H - 2][:, s, frames],
+                        rhs=codes_u[:, s, :].bitcast(FP8X4),
+                        rhs_scale=scales_u[:, s, :],
+                        start=(s == 0),
+                        stop=(s == PASSES - 1),
+                    )
+            return accs
+
+        def late_store(u, accs):
+            for half in range(2):
+                scaled = out_pool.tile([P, 2, P], F32, tag="scaled")
+                if half == 0:
+                    nc.scalar.mul(out=scaled[:], in_=accs[half][:], mul=1.0 / math.sqrt(K))
+                else:
+                    nc.vector.tensor_scalar_mul(out=scaled[:], in0=accs[half][:], scalar1=1.0 / math.sqrt(K))
+                nc.sync.dma_start(
+                    out=out[0, H - 1, half * 2 * P : (half + 1) * 2 * P, (u - k3) * P : (u - k3 + 1) * P].rearrange(
+                        "(q p) t -> p q t", p=P
+                    ),
+                    in_=scaled[:],
+                )
+
+        def stage_turn(k):
+            if k < k3:
+                turn(k)
+            elif k < UNITS:
+                late_turn(k)
+
+        def stage_gain(k):
+            if k < k3:
+                for j in range(PACK):
+                    gain_shift(k, j, j % 2 == 1)
+            elif k < UNITS:
+                for s in range(PASSES):
+                    for j in range(PACK):
+                        late_gain(k, s, j, s % 2 == 1)
+
+        def stage_regroup(k):
+            if k < k3:
+                regroup(k, "scalar", T // 2)
+            elif k < UNITS:
+                late_regroup(k)
+
+        def stage_quantise(k):
+            if k < k3:
+                quantise_pass(k)
+            elif k < UNITS:
+                late_quantise(k)
+
+
         with tc.manual_schedule():
             conv_banks = convolve(0)
-            for n in range(UNITS + LAG_TURN + 2):
+            for n in range(UNITS):
                 b = n - LAG_TURN
-                vector_is_free = n >= UNITS
-                u_norm = n - 1 - LAG_STAT
-                r = b - 6
-                scores_due = 0 <= r < UNITS - FRAME_TILES and (r // FRAME_TILES) % 2 == 1
-                if 0 <= u_norm < UNITS:
-                    normalise(u_norm, nc.vector if vector_is_free else nc.gpsimd)
+                final = n == UNITS - 1
+                half = n - LAG_TURN - 2 - 2 * FRAME_TILES
+                if n >= 2:
+                    normalise(n - 2, nc.gpsimd)
                 early = n < LAG_TURN
-                if 0 <= n - 1 < UNITS and not early:
+                if n > 0 and not early:
                     squares(n - 1)
-                if 0 <= b - 1 < UNITS - 1:
-                    regroup(b - 1, "gpsimd", SPLIT_END if vector_is_free else SPLIT)
-                if 0 <= n - 1 < UNITS and not early:
+                if b >= 1:
+                    regroup(b - 1, "gpsimd", SPLIT)
+                if n > 0 and not early:
                     inverse_deviation(n - 1)
-                if scores_due and not vector_is_free:
-                    acc = turn_psum.tile([P, T], F32, tag="turned")
-                    score_passes(r // (2 * FRAME_TILES), r % FRAME_TILES, acc, range(PASSES))
-                if 0 <= b < UNITS:
+                if half >= 0:
+                    h, half_tt = half // 8, half % 8 // 2
+                    keys = slice((half % 2) * (T // 2), (half % 2 + 1) * (T // 2))
+                    acc = turn_psum.tile([P, T // 2], F32, tag="turned")
+                    score_passes(h, half_tt, acc, range(PASSES), keys)
+                if n == 3:
+                    finish_tables()
+
+                def stats():
+                    if n > 0:
+                        squares(n - 1)
+                        inverse_deviation(n - 1)
+
+                prelu(n, conv_banks, 1 if early else 0, stats if early else None,
+                      (lambda: release(n - 1)) if final else None)
+                if b >= 0:
                     planes_b = work_pool.tile([P, PACK, T], BF16, bufs=3)
                     planes[b] = planes_b
                     turned_banks = turn(b)
-                if n == 3:
-                    finish_tables()
-                if n < UNITS:
-                    def stats():
-                        if n > 0:
-                            squares(n - 1)
-                            inverse_deviation(n - 1)
-                    prelu(n, conv_banks, 1 if early else 0, stats if early else None)
                 if n + 1 < UNITS:
                     conv_banks = convolve(n + 1)
-                if scores_due and not vector_is_free:
-                    store_scores(r // (2 * FRAME_TILES), r % FRAME_TILES, acc, False)
-                if 0 <= b < UNITS:
+                if half >= 0:
+                    store_scores(h, half_tt, acc, False, keys)
+                if b >= 0:
                     gain_shift(b, 0, turned_banks[0], False)
                 if n == 0:
                     copy_x(0, 0, F // 2)
                     copy_x(1, 0, F // 4)
                 elif n + 2 < 2 * FRAME_TILES:
                     copy_x((n + 2) // 2, (n + 2) % 2 * (F // 4), F // 4)
-                if 0 <= b < UNITS:
-                    gain_shift(b, 1, turned_banks[1], vector_is_free)
+                if b >= 0:
+                    if not final:
+                        gain_shift(b, 1, turned_banks[1], False)
                     gain_shift(b, 2, turned_banks[2], False)
-                    gain_shift(b, 3, turned_banks[3], vector_is_free)
-                if b - 1 == UNITS - 1:
-                    regroup(b - 1, "scalar", T // 2)
+                    if not final:
+                        gain_shift(b, 3, turned_banks[3], False)
                 if n == 1:
                     cast_tables()
                 if n == 2:
                     turn_tables()
-                if 0 <= n - LAG_STAT < UNITS:
-                    release(n - LAG_STAT)
-                if 0 <= b - 2 < UNITS:
-                    quantise_pass(b - 2)
-                if n < UNITS:
+                if final:
                     sum_parts(n)
-                if scores_due and vector_is_free:
-                    acc = conv_psum.tile([P, T], F32, tag="conv")
-                    score_passes(r // (2 * FRAME_TILES), r % FRAME_TILES, acc, range(PASSES))
-                    store_scores(r // (2 * FRAME_TILES), r % FRAME_TILES, acc, r % 2 == 1)
-                if UNITS - PASSES <= b - 2 < UNITS:
-                    for tt in range(FRAME_TILES):
-                        if b - 2 == UNITS - PASSES:
-                            acc = conv_psum.tile([P, T], F32, tag="conv")
-                            last_acc.append(acc)
-                        score_passes(H - 1, tt, last_acc[tt], ((b - 2) % PASSES,))
-                if b - 2 == UNITS - 1:
-                    for tt in range(FRAME_TILES):
-                        store_scores(H - 1, tt, last_acc[tt], tt % 2 == 1)
+                    gain_shift(b, 1, turned_banks[1], True)
+                    gain_shift(b, 3, turned_banks[3], True)
+                    quantise_pass(b - 2)
+                    quantise_pass(b - 1)
+                else:
+                    if n > 0:
+                        release(n - 1)
+                    if b >= 2:
+                        quantise_pass(b - 2)
+                    sum_parts(n)
+            first_late = UNITS - LAG_TURN
+            late_banks = {}
+            normalise(UNITS - 2, nc.gpsimd)
+            squares(UNITS - 1)
+            inverse_deviation(UNITS - 1)
+            accs = {}
+            for k in range(first_late, UNITS + 3):
+                if k < k3:
+                    planes_b = work_pool.tile([P, PACK, T], BF16, bufs=3)
+                    planes[k] = planes_b
+                    late_banks[k] = turn(k)
+                elif k < UNITS:
+                    late_turn(k)
+                copies = head2_scores(({0: 3, 1: 2, 2: 2}).get(k - first_late, 0))
+                if k3 <= k - 2 < UNITS:
+                    accs[k - 2] = late_scores(k - 2)
+                if k == first_late + 1:
+                    release(UNITS - 1)
+                    normalise(UNITS - 1, nc.vector)
+                if k - 1 < k3:
+                    regroup(k - 1, "scalar", T // 2)
+                elif k - 1 < UNITS:
+                    late_regroup(k - 1)
+                if k < k3:
+                    for j in range(PACK):
+                        gain_shift(k, j, late_banks[k][j], j % 2 == 1)
+                elif k < UNITS:
+                    for s in range(PASSES):
+                        for j in range(PACK):
+                            late_gain(k, s, j, s % 2 == 1)
+                if k - 1 < k3:
+                    quantise_pass(k - 1)
+                elif k - 1 < UNITS:
+                    late_quantise(k - 1)
+                for tt, acc, keys in copies:
+                    store_scores(2, tt, acc, keys.start == 0, keys)
+                if k3 <= k - 2 < UNITS:
+                    late_store(k - 2, accs[k - 2])

@@ -228,7 +228,7 @@ def tile_multiheadselfattention_pa_kernel(
                         stop=(f8 == OCT - 1),
                     )
 
-        def prelu(u, banks, scalar_banks, between, before_last=None):
+        def prelu(u, banks, scalar_banks):
             g = group_of(u)
             feat_u = feat_pool.tile([P, K], F32)
             feat[u] = feat_u
@@ -258,15 +258,11 @@ def tile_multiheadselfattention_pa_kernel(
 
             for j in range(PACK - scalar_banks, PACK):
                 times_slope(j)
-            if between is not None:
-                between()
             times_slope(0)
             for j in range(1, PACK):
                 if j < PACK - scalar_banks:
                     times_slope(j)
                 larger(j - 1)
-                if j == 2 and before_last is not None:
-                    before_last()
             larger(PACK - 1)
 
         def sum_parts(u):
@@ -462,7 +458,7 @@ def tile_multiheadselfattention_pa_kernel(
             for s in range(PASSES):
                 o = grouped_u[:, s, :, :].rearrange("p (c i) j -> p c j i", i=4)
                 i = late[u][0][:, s, :, :].rearrange("p j (c i) -> p c j i", i=4)
-                if s < 2:
+                if s < (1 if u == UNITS - 1 else 2):
                     nc.scalar.copy(out=o, in_=i)
                 else:
                     nc.vector.tensor_copy(out=o, in_=i)
@@ -548,12 +544,14 @@ def tile_multiheadselfattention_pa_kernel(
                 if n >= 2:
                     normalise(n - 2, nc.gpsimd)
                 early = n < LAG_TURN
-                if n > 0 and not early:
+                if n > 0:
                     squares(n - 1)
                 if b >= 1:
                     regroup(b - 1, "gpsimd", SPLIT)
-                if n > 0 and not early:
+                if n > 0:
                     inverse_deviation(n - 1)
+                if n == 0:
+                    copy_x(0, 0, F // 2)
                 if half >= 0:
                     h, half_tt = half // 8, half % 8 // 2
                     keys = slice((half % 2) * (T // 2), (half % 2 + 1) * (T // 2))
@@ -562,13 +560,7 @@ def tile_multiheadselfattention_pa_kernel(
                 if n == 3:
                     finish_tables()
 
-                def stats():
-                    if n > 0:
-                        squares(n - 1)
-                        inverse_deviation(n - 1)
-
-                prelu(n, conv_banks, 1 if early else 0, stats if early else None,
-                      (lambda: release(n - 1)) if final else None)
+                prelu(n, conv_banks, 1 if early else 0)
                 if b >= 0:
                     planes_b = work_pool.tile([P, PACK, T], BF16, bufs=3)
                     planes[b] = planes_b
@@ -579,10 +571,7 @@ def tile_multiheadselfattention_pa_kernel(
                     store_scores(h, half_tt, acc, False, keys)
                 if b >= 0:
                     gain_shift(b, 0, turned_banks[0], False)
-                if n == 0:
-                    copy_x(0, 0, F // 2)
-                    copy_x(1, 0, F // 4)
-                elif n + 2 < 2 * FRAME_TILES:
+                if n + 2 < 2 * FRAME_TILES:
                     copy_x((n + 2) // 2, (n + 2) % 2 * (F // 4), F // 4)
                 if b >= 0:
                     if not final:
@@ -598,6 +587,7 @@ def tile_multiheadselfattention_pa_kernel(
                     sum_parts(n)
                     gain_shift(b, 1, turned_banks[1], True)
                     gain_shift(b, 3, turned_banks[3], True)
+                    release(n - 1)
                     quantise_pass(b - 2)
                     quantise_pass(b - 1)
                 else:

import math
from contextlib import ExitStack

import concourse.mybir as mybir
from concourse.masks import make_identity

F32 = mybir.dt.float32
BF16 = mybir.dt.bfloat16
U32 = mybir.dt.uint32
U8 = mybir.dt.uint8
FP8X4 = mybir.dt.float8_e4m3fn_x4
ALU = mybir.AluOpType
ACT = mybir.ActivationFunctionType

P = 128
C = 128
T = 512
F = 32
H = 4
D = 64
K = D * F
EPS = 1e-5
G = 2 * H
FRAME_TILES = T // P
PACK = 4
K_PASS = P * PACK
PASSES = K // K_PASS
OCT = F // PACK
UNITS = G * FRAME_TILES
LAG_TURN = 5
LAG_STAT = 1
FEAT_BUFS = 12
SPLIT = 416
SPLIT_END = 320

FLOPS = 2 * C * (G * D) * (T * F) + 2 * H * T * T * K


def tile_multiheadselfattention_pa_kernel(
    tc, x, Wq, bq, aq, lwq, lbq, Wk, bk, ak, lwk, lbk, out
):
    nc = tc.nc
    with ExitStack() as ctx:
        const = ctx.enter_context(tc.tile_pool(name="const", bufs=1))
        feat_pool = ctx.enter_context(tc.tile_pool(name="feat", bufs=FEAT_BUFS))
        stat_pool = ctx.enter_context(tc.tile_pool(name="stat", bufs=8))
        work_pool = ctx.enter_context(tc.tile_pool(name="work", bufs=2))
        code_pool = ctx.enter_context(tc.tile_pool(name="code", bufs=4))
        out_pool = ctx.enter_context(tc.tile_pool(name="outp", bufs=FRAME_TILES))
        conv_psum = ctx.enter_context(tc.psum_pool(name="convp", bufs=4))
        turn_psum = ctx.enter_context(tc.psum_pool(name="turnp", bufs=4))

        bias_rows_bf = const.tile([P, D], BF16)
        nc.vector.memset(bias_rows_bf[:], 0.0)
        nc.sync.dma_start(out=bias_rows_bf[0:H, :], in_=bq)
        nc.sync.dma_start(out=bias_rows_bf[H:G, :], in_=bk)
        ident_f32 = const.tile([P, P], F32)
        make_identity(nc, ident_f32[:])
        ident_bf = const.tile([P, P], BF16)
        make_identity(nc, ident_bf[:])

        zero_col = const.tile([P, 1], F32)
        nc.vector.memset(zero_col[:], 0.0)
        eps_col = const.tile([P, 1], F32)
        nc.vector.tensor_scalar_add(out=eps_col[:], in0=zero_col[:], scalar1=EPS)

        slope_q = const.tile([P, H], BF16)
        nc.scalar.dma_start(out=slope_q[:], in_=aq.partition_broadcast(P))
        slope_k = const.tile([P, H], BF16)
        nc.scalar.dma_start(out=slope_k[:], in_=ak.partition_broadcast(P))
        table_col = const.tile([P, 1], F32)
        nc.scalar.activation(
            out=table_col[:], in_=zero_col[:], func=ACT.Abs_reciprocal_sqrt, bias=eps_col[:], scale=1.0
        )

        slope = const.tile([P, G], F32)
        nc.vector.tensor_copy(out=slope[:, 0:H], in_=slope_q[:])
        nc.vector.tensor_copy(out=slope[:, H:G], in_=slope_k[:])

        sign = const.tile([P, G], F32)
        nc.vector.tensor_scalar(
            out=sign[:], in0=slope[:], scalar1=1.0, scalar2=-2.0, op0=ALU.is_gt, op1=ALU.mult
        )
        nc.vector.tensor_scalar_add(out=sign[:], in0=sign[:], scalar1=1.0)

        first_sign = const.tile([P, 1], BF16)
        nc.vector.tensor_tensor(out=first_sign[:], in0=ident_bf[:, 0:1], in1=sign[:, 0:1], op=ALU.mult)

        w_rows = const.tile([P, 4, C], BF16)
        nc.sync.dma_start(out=w_rows[:, 0:2, :], in_=Wq.rearrange("(a h) d c -> (h d) a c", a=2))
        nc.sync.dma_start(out=w_rows[:, 2:4, :], in_=Wk.rearrange("(a h) d c -> (h d) a c", a=2))
        w_turned = turn_psum.tile([P, 4, P], BF16, tag="turned")
        for i in range(4):
            nc.tensor.transpose(w_turned[:, i, :], w_rows[:, i, :], ident_bf[:])
        w_T = const.tile([P, G, D], BF16)
        nc.vector.tensor_tensor(
            out=w_T[:],
            in0=w_turned[:].rearrange("c i (h d) -> c (i h) d", d=D),
            in1=sign[:].unsqueeze(2).to_broadcast([P, G, D]),
            op=ALU.mult,
        )

        x_ft = const.tile([P, F // 2, T, 2], BF16)
        x_raw = []
        for tt in range(FRAME_TILES):
            raw = feat_pool.tile([P, P, F], BF16, tag="feat_u")
            nc.sync.dma_start(out=raw[:], in_=x[0, :, tt * P : (tt + 1) * P, :])
            x_raw.append(raw)

        bias_rows = const.tile([P, P], F32)
        for twice in range(2):
            nc.vector.tensor_copy(out=bias_rows[:, twice * D : (twice + 1) * D], in_=bias_rows_bf[:])
        bias_turned = turn_psum.tile([P, P], F32, tag="turned")
        nc.tensor.transpose(bias_turned[:], bias_rows[:], ident_f32[:])
        bias_col = const.tile([P, G], F32)
        nc.vector.tensor_tensor(out=bias_col[:], in0=bias_turned[:, 0:G], in1=sign[:], op=ALU.mult)

        gain_rows_bf = const.tile([P, P], BF16)
        shift_rows_bf = const.tile([P, P], BF16)
        for side, (lw, lb) in enumerate(((lwq, lbq), (lwk, lbk))):
            for rows_bf, table in ((gain_rows_bf, lw), (shift_rows_bf, lb)):
                by_j = table.rearrange("h (s d) (j f) -> j (h s) d f", s=PASSES, j=PACK)
                for j in range(PACK):
                    nc.sync.dma_start(
                        out=rows_bf[side * 64 + j : (side + 1) * 64 : PACK, :].rearrange(
                            "r (d f) -> r d f", f=OCT
                        ),
                        in_=by_j[j],
                    )
        gain_rows = const.tile([P, P], F32)
        shift_rows = const.tile([P, P], F32)
        gain_T = const.tile([P, G, PASSES * PACK], F32)
        shift_T = const.tile([P, G, PASSES * PACK], F32)
        tables = []

        def cast_tables():
            for rows, rows_bf in ((gain_rows, gain_rows_bf), (shift_rows, shift_rows_bf)):
                nc.gpsimd.tensor_scalar(
                    out=rows[:], in0=rows_bf[:], scalar1=1.0, scalar2=0.0, op0=ALU.mult, op1=ALU.add
                )

        def turn_tables():
            table_turned = conv_psum.tile([P, 2, P], F32, tag="conv")
            nc.tensor.transpose(table_turned[:, 0, :], gain_rows[:], ident_f32[:])
            nc.tensor.transpose(table_turned[:, 1, :], shift_rows[:], ident_f32[:])
            tables.append(table_turned)

        def finish_tables():
            nc.vector.tensor_tensor(
                out=gain_T[:],
                in0=tables[0][:, 0, :].rearrange("p (g c) -> p g c", g=G),
                in1=sign[:].unsqueeze(2).to_broadcast([P, G, PASSES * PACK]),
                op=ALU.mult,
            )
            nc.vector.tensor_copy(
                out=shift_T[:], in_=tables[0][:, 1, :].rearrange("p (g c) -> p g c", g=G)
            )

        feat = {}
        parts = {}
        total = {}
        sq_total = {}
        rstd = {}
        offset = {}
        planes = {}
        grouped = {}
        codes = {}
        scales = {}

        def group_of(u):
            i = u // FRAME_TILES
            return (i % 2) * H + i // 2

        def copy_x(tt, first, count):
            nc.scalar.copy(
                out=x_ft[:, first : first + count, tt * P : (tt + 1) * P, :]
                .rearrange("c f t e -> c f (t e)")
                .bitcast(F32)
                .rearrange("c (q i) t -> c q t i", i=4),
                in_=x_raw[tt][:].bitcast(F32)[:, :, first : first + count].rearrange("c t (q i) -> c q t i", i=4),
            )

        def convolve(u):
            g = group_of(u)
            banks = []
            for j in range(PACK):
                if u < LAG_TURN and u % 2 == 1:
                    conv = turn_psum.tile([P, OCT, D], F32, tag="turned")
                else:
                    conv = conv_psum.tile([P, OCT, D], F32, tag="conv")
                banks.append(conv)
                if u == 0 and j >= 2:
                    convolve_bank(u, j - 2, banks[j - 2])
                if u < FRAME_TILES:
                    nc.tensor.matmul(
                        out=conv[:],
                        lhsT=first_sign[:].to_broadcast([P, P]),
                        rhs=bias_rows_bf[:].unsqueeze(1).to_broadcast([P, OCT, D]),
                        start=True,
                        stop=False,
                    )
                else:
                    for quarter in range(K_PASS // P):
                        nc.tensor.matmul(
                            out=conv[:, 2 * quarter : 2 * quarter + 2, :].rearrange("p f d -> p (f d)"),
                            lhsT=bias_col[:, g : g + 1].to_broadcast([P, P]),
                            rhs=ident_f32[:],
                            is_transpose=True,
                            start=(quarter == 0),
                            stop=False,
                        )
                if u > 0:
                    convolve_bank(u, j, conv)
            if u == 0:
                convolve_bank(u, 2, banks[2])
                convolve_bank(u, 3, banks[3])
            return banks

        def convolve_bank(u, j, conv):
                g, tt = group_of(u), u % FRAME_TILES
                frames = slice(tt * P, (tt + 1) * P)
                for f8 in range(OCT):
                    nc.tensor.matmul(
                        out=conv[:, f8, :],
                        lhsT=(x_raw[tt][:, :, j * OCT + f8] if u < FRAME_TILES else x_ft[:, (j * OCT + f8) // 2, frames, f8 % 2]),
                        rhs=w_T[:, g, :],
                        start=False,
                        stop=(f8 == OCT - 1),
                    )

        def prelu(u, banks, scalar_banks):
            g = group_of(u)
            feat_u = feat_pool.tile([P, K], F32)
            feat[u] = feat_u
            parts_u = stat_pool.tile([P, PACK], F32)
            parts[u] = parts_u
            scaled_v = [None] * PACK

            def times_slope(j):
                a_v = work_pool.tile([P, D, OCT], F32, bufs=4)
                v = banks[j][:].rearrange("p f d -> p d f")
                if j < PACK - scalar_banks:
                    nc.vector.tensor_scalar_mul(out=a_v[:], in0=v, scalar1=slope[:, g : g + 1])
                else:
                    nc.scalar.activation(out=a_v[:], in_=v, func=ACT.Copy, scale=slope[:, g : g + 1])
                scaled_v[j] = a_v

            def larger(j):
                nc.vector.scalar_tensor_tensor(
                    out=feat_u[:, j * K_PASS : (j + 1) * K_PASS].rearrange("p (d f) -> p d f", f=OCT),
                    in0=banks[j][:].rearrange("p f d -> p d f"),
                    scalar=1.0,
                    in1=scaled_v[j][:],
                    op0=ALU.mult,
                    op1=ALU.max,
                    accum_out=parts_u[:, j : j + 1],
                )

            for j in range(PACK - scalar_banks, PACK):
                times_slope(j)
            times_slope(0)
            for j in range(1, PACK):
                if j < PACK - scalar_banks:
                    times_slope(j)
                larger(j - 1)
            larger(PACK - 1)

        def sum_parts(u):
            total_u = stat_pool.tile([P, 1], F32)
            total[u] = total_u
            nc.vector.tensor_reduce(out=total_u[:], in_=parts[u][:], axis=mybir.AxisListType.X, op=ALU.add)

        def squares(u):
            sq_u = stat_pool.tile([P, 1], F32)
            sq_total[u] = sq_u
            junk = work_pool.tile([P, K], BF16, bufs=1)
            nc.scalar.activation(
                out=junk[:],
                in_=feat[u][:],
                func=ACT.Square,
                bias=total[u][:],
                scale=-1.0 * K,
                accum_out=sq_u[:],
            )

        def inverse_deviation(u):
            rstd_u = stat_pool.tile([P, 1], F32)
            rstd[u] = rstd_u
            nc.scalar.activation(
                out=rstd_u[:],
                in_=sq_total[u][:],
                func=ACT.Abs_reciprocal_sqrt,
                bias=eps_col[:],
                scale=1.0 / (K * K * K),
            )

        def release(u):
            offset_u = stat_pool.tile([P, 1], F32)
            offset[u] = offset_u
            nc.vector.tensor_scalar(
                out=offset_u[:],
                in0=total[u][:],
                scalar1=rstd[u][:],
                scalar2=-1.0 / K,
                op0=ALU.mult,
                op1=ALU.mult,
            )

        def normalise(u, engine):
            engine.tensor_scalar(
                out=feat[u][:],
                in0=feat[u][:],
                scalar1=rstd[u][:],
                scalar2=offset[u][:],
                op0=ALU.mult,
                op1=ALU.add,
            )

        def turn(b):
            i, s = b // PASSES, b % PASSES
            banks = []
            for j in range(PACK):
                turned = turn_psum.tile([P, T], F32)
                first = j * K_PASS + s * P
                for tt in range(FRAME_TILES):
                    nc.tensor.transpose(
                        turned[:, tt * P : (tt + 1) * P],
                        feat[i * FRAME_TILES + tt][:, first : first + P],
                        ident_f32[:],
                    )
                banks.append(turned)
            return banks

        def gain_shift(b, j, turned, on_vector):
            g, s = group_of(b), b % PASSES
            col = s * PACK + j
            if on_vector:
                nc.vector.tensor_scalar(
                    out=planes[b][:, j, :],
                    in0=turned[:],
                    scalar1=gain_T[:, g, col : col + 1],
                    scalar2=shift_T[:, g, col : col + 1],
                    op0=ALU.mult,
                    op1=ALU.add,
                )
            else:
                nc.scalar.activation(
                    out=planes[b][:, j, :],
                    in_=turned[:],
                    func=ACT.Identity,
                    bias=shift_T[:, g, col : col + 1],
                    scale=gain_T[:, g, col : col + 1],
                )

        def regroup(b, first_engine, split):
            if b % 2 == 0:
                pair = work_pool.tile([P, 2, T, PACK], BF16, align_bytes=64)
                grouped[b // 2] = pair
            pair = grouped[b // 2]
            low_out = pair[:, b % 2, 0:split, :].rearrange("p (c i) j -> p c j i", i=4)
            low_in = planes[b][:, :, 0:split].rearrange("p j (c i) -> p c j i", i=4)
            high_out = pair[:, b % 2, split:T, :].rearrange("p (c i) j -> p c j i", i=4)
            high_in = planes[b][:, :, split:T].rearrange("p j (c i) -> p c j i", i=4)
            if first_engine == "gpsimd":
                nc.gpsimd.tensor_scalar(
                    out=pair[:, b % 2, 0:split, :],
                    in0=planes[b][:, :, 0:split].rearrange("p j t -> p t j"),
                    scalar1=1.0,
                    scalar2=0.0,
                    op0=ALU.mult,
                    op1=ALU.add,
                )
                nc.scalar.copy(out=high_out, in_=high_in)
            else:
                nc.scalar.copy(out=low_out, in_=low_in)
                nc.vector.tensor_copy(out=high_out, in_=high_in)

        def quantise_pass(b):
            i, s = b // PASSES, b % PASSES
            if s == 0:
                codes_i = code_pool.tile([P, PASSES, T], U32, align_bytes=64)
                scales_i = code_pool.tile([P, PASSES, T], U8, align_bytes=64)
                codes[i] = codes_i
                scales[i] = scales_i
            nc.vector.quantize_mx(
                out=codes[i][:, s, :].bitcast(FP8X4),
                scales=scales[i][:, s, :],
                in_=grouped[b // 2][:, b % 2, :, :].rearrange("p t j -> p (t j)"),
            )

        def score_passes(h, tt, acc, passes, keys=slice(0, T)):
            frames = slice(tt * P, (tt + 1) * P)
            for s in passes:
                nc.tensor.matmul_mx(
                    out=acc[:],
                    lhsT=codes[2 * h][:, s, frames].bitcast(FP8X4),
                    lhsT_scale=scales[2 * h][:, s, frames],
                    rhs=codes[2 * h + 1][:, s, keys].bitcast(FP8X4),
                    rhs_scale=scales[2 * h + 1][:, s, keys],
                    start=(s == 0),
                    stop=(s == PASSES - 1),
                )

        def store_scores(h, tt, acc, on_vector, keys=slice(0, T)):
            frames = slice(tt * P, (tt + 1) * P)
            scaled = out_pool.tile([P, keys.stop - keys.start], F32)
            if on_vector:
                nc.vector.tensor_scalar_mul(out=scaled[:], in0=acc[:], scalar1=1.0 / math.sqrt(K))
            else:
                nc.scalar.mul(out=scaled[:], in_=acc[:], mul=1.0 / math.sqrt(K))
            nc.sync.dma_start(out=out[0, h, frames, keys], in_=scaled[:])

        k3 = (G - 1) * PASSES
        late = {}
        late_codes = {}
        halves = list(range(1, 8))

        def head2_scores(count):
            accs = []
            for x in halves[:count]:
                tt, keys = x // 2, slice(x % 2 * (T // 2), x % 2 * (T // 2) + (T // 2))
                acc = conv_psum.tile([P, (T // 2)], F32, tag="conv")
                score_passes(2, tt, acc, range(PASSES), keys)
                accs.append((tt, acc, keys))
            for i in range(len(accs)):
                halves.remove(halves[0])
            return accs

        def late_turn(u):
            planes_u = work_pool.tile([P, PASSES, PACK, P], BF16, tag="planes_b", bufs=3)
            banks = []
            for s in range(PASSES):
                turned = turn_psum.tile([P, PACK, P], F32, tag="turned")
                for j in range(PACK):
                    first = j * K_PASS + s * P
                    nc.tensor.transpose(turned[:, j, :], feat[u][:, first : first + P], ident_f32[:])
                banks.append(turned)
            late[u] = (planes_u, banks)

        def late_gain(u, s, j, on_vector):
            planes_u, banks = late[u]
            g, col = group_of(u), s * PACK + j
            if on_vector:
                nc.vector.tensor_scalar(
                    out=planes_u[:, s, j, :], in0=banks[s][:, j, :],
                    scalar1=gain_T[:, g, col : col + 1], scalar2=shift_T[:, g, col : col + 1],
                    op0=ALU.mult, op1=ALU.add,
                )
            else:
                nc.scalar.activation(
                    out=planes_u[:, s, j, :], in_=banks[s][:, j, :], func=ACT.Identity,
                    bias=shift_T[:, g, col : col + 1], scale=gain_T[:, g, col : col + 1],
                )

        def late_regroup(u):
            grouped_u = work_pool.tile([P, PASSES, P, PACK], BF16, tag="pair", align_bytes=64)
            grouped[u] = grouped_u
            for s in range(PASSES):
                o = grouped_u[:, s, :, :].rearrange("p (c i) j -> p c j i", i=4)
                i = late[u][0][:, s, :, :].rearrange("p j (c i) -> p c j i", i=4)
                if s < (1 if u == UNITS - 1 else 2):
                    nc.scalar.copy(out=o, in_=i)
                else:
                    nc.vector.tensor_copy(out=o, in_=i)

        def late_quantise(u):
            codes_u = code_pool.tile([P, PASSES, P], U32, tag="codes_u", bufs=2, align_bytes=64)
            scales_u = code_pool.tile([P, PASSES, P], U8, tag="scales_u", bufs=2, align_bytes=64)
            nc.vector.quantize_mx(
                out=codes_u[:].rearrange("p s t -> p (s t)").bitcast(FP8X4),
                scales=scales_u[:].rearrange("p s t -> p (s t)"),
                in_=grouped[u][:].rearrange("p s t j -> p (s t j)"),
            )
            late_codes[u] = (codes_u, scales_u)

        def late_scores(u):
            codes_u, scales_u = late_codes[u]
            accs = []
            for tt in range(FRAME_TILES):
                if tt % 2 == 0:
                    acc = conv_psum.tile([P, 2, P], F32, tag="conv")
                    accs.append(acc)
                frames = slice(tt * P, (tt + 1) * P)
                for s in range(PASSES):
                    nc.tensor.matmul_mx(
                        out=acc[:, tt % 2, :],
                        lhsT=codes[2 * H - 2][:, s, frames].bitcast(FP8X4),
                        lhsT_scale=scales[2 * H - 2][:, s, frames],
                        rhs=codes_u[:, s, :].bitcast(FP8X4),
                        rhs_scale=scales_u[:, s, :],
                        start=(s == 0),
                        stop=(s == PASSES - 1),
                    )
            return accs

        def late_store(u, accs):
            for half in range(2):
                scaled = out_pool.tile([P, 2, P], F32, tag="scaled")
                if half == 0:
                    nc.scalar.mul(out=scaled[:], in_=accs[half][:], mul=1.0 / math.sqrt(K))
                else:
                    nc.vector.tensor_scalar_mul(out=scaled[:], in0=accs[half][:], scalar1=1.0 / math.sqrt(K))
                nc.sync.dma_start(
                    out=out[0, H - 1, half * 2 * P : (half + 1) * 2 * P, (u - k3) * P : (u - k3 + 1) * P].rearrange(
                        "(q p) t -> p q t", p=P
                    ),
                    in_=scaled[:],
                )

        def stage_turn(k):
            if k < k3:
                turn(k)
            elif k < UNITS:
                late_turn(k)

        def stage_gain(k):
            if k < k3:
                for j in range(PACK):
                    gain_shift(k, j, j % 2 == 1)
            elif k < UNITS:
                for s in range(PASSES):
                    for j in range(PACK):
                        late_gain(k, s, j, s % 2 == 1)

        def stage_regroup(k):
            if k < k3:
                regroup(k, "scalar", T // 2)
            elif k < UNITS:
                late_regroup(k)

        def stage_quantise(k):
            if k < k3:
                quantise_pass(k)
            elif k < UNITS:
                late_quantise(k)


        with tc.manual_schedule():
            conv_banks = convolve(0)
            for n in range(UNITS):
                b = n - LAG_TURN
                final = n == UNITS - 1
                half = n - LAG_TURN - 2 - 2 * FRAME_TILES
                if n >= 2:
                    normalise(n - 2, nc.gpsimd)
                early = n < LAG_TURN
                if n > 0:
                    squares(n - 1)
                if b >= 1:
                    regroup(b - 1, "gpsimd", SPLIT)
                if n > 0:
                    inverse_deviation(n - 1)
                if n == 0:
                    copy_x(0, 0, F // 2)
                if half >= 0:
                    h, half_tt = half // 8, half % 8 // 2
                    keys = slice((half % 2) * (T // 2), (half % 2 + 1) * (T // 2))
                    acc = turn_psum.tile([P, T // 2], F32, tag="turned")
                    score_passes(h, half_tt, acc, range(PASSES), keys)
                if n == 3:
                    finish_tables()

                prelu(n, conv_banks, 1 if early else 0)
                if b >= 0:
                    planes_b = work_pool.tile([P, PACK, T], BF16, bufs=3)
                    planes[b] = planes_b
                    turned_banks = turn(b)
                if n + 1 < UNITS:
                    conv_banks = convolve(n + 1)
                if half >= 0:
                    store_scores(h, half_tt, acc, False, keys)
                if b >= 0:
                    gain_shift(b, 0, turned_banks[0], False)
                if n + 2 < 2 * FRAME_TILES:
                    copy_x((n + 2) // 2, (n + 2) % 2 * (F // 4), F // 4)
                if b >= 0:
                    if not final:
                        gain_shift(b, 1, turned_banks[1], False)
                    gain_shift(b, 2, turned_banks[2], False)
                    if not final:
                        gain_shift(b, 3, turned_banks[3], False)
                if n == 1:
                    cast_tables()
                if n == 2:
                    turn_tables()
                if final:
                    sum_parts(n)
                    gain_shift(b, 1, turned_banks[1], True)
                    gain_shift(b, 3, turned_banks[3], True)
                    release(n - 1)
                    quantise_pass(b - 2)
                    quantise_pass(b - 1)
                else:
                    if n > 0:
                        release(n - 1)
                    if b >= 2:
                        quantise_pass(b - 2)
                    sum_parts(n)
            first_late = UNITS - LAG_TURN
            late_banks = {}
            normalise(UNITS - 2, nc.gpsimd)
            squares(UNITS - 1)
            inverse_deviation(UNITS - 1)
            accs = {}
            for k in range(first_late, UNITS + 3):
                if k < k3:
                    planes_b = work_pool.tile([P, PACK, T], BF16, bufs=3)
                    planes[k] = planes_b
                    late_banks[k] = turn(k)
                elif k < UNITS:
                    late_turn(k)
                copies = head2_scores(({0: 3, 1: 2, 2: 2}).get(k - first_late, 0))
                if k3 <= k - 2 < UNITS:
                    accs[k - 2] = late_scores(k - 2)
                if k == first_late + 1:
                    release(UNITS - 1)
                    normalise(UNITS - 1, nc.vector)
                if k - 1 < k3:
                    regroup(k - 1, "scalar", T // 2)
                elif k - 1 < UNITS:
                    late_regroup(k - 1)
                if k < k3:
                    for j in range(PACK):
                        gain_shift(k, j, late_banks[k][j], j % 2 == 1)
                elif k < UNITS:
                    for s in range(PASSES):
                        for j in range(PACK):
                            late_gain(k, s, j, s % 2 == 1)
                if k - 1 < k3:
                    quantise_pass(k - 1)
                elif k - 1 < UNITS:
                    late_quantise(k - 1)
                for tt, acc, keys in copies:
                    store_scores(2, tt, acc, keys.start == 0, keys)
                if k3 <= k - 2 < UNITS:
                    late_store(k - 2, accs[k - 2])
